import numpy as np
import ml_dtypes


def mxq(x, axis, fmt="e4m3"):
    dtype, down = {"e4m3": (ml_dtypes.float8_e4m3fn, 7), "e5m2": (ml_dtypes.float8_e5m2, 14)}[fmt]
    v = np.moveaxis(np.asarray(x, np.float32).astype(ml_dtypes.bfloat16).astype(np.float64), axis, -1)
    blocks = v.reshape(v.shape[:-1] + (-1, 32))
    amax = np.abs(blocks).max(-1, keepdims=True)
    byte = np.maximum(np.where(amax > 0, np.frexp(amax)[1] - 1 + 127, 0) - down, 1)
    scale = np.exp2(byte - 127.0)
    codes = (blocks / scale).astype(np.float32).astype(dtype).astype(np.float64)
    return np.moveaxis((codes * scale).reshape(v.shape), -1, axis)


WIDE = False


def mx_kscale(k):
    if not WIDE:
        return np.ones(k)
    levels = np.array([10, -10, 5, -5, 0])
    a = np.random.permutation(np.resize(levels, k // 512 * 4)).reshape(k // 512, 4)
    idx = np.arange(k)
    return np.exp2(a[idx // 512, idx % 128 // 32])


BF16 = ml_dtypes.bfloat16


def bf(x):
    return np.asarray(x, np.float32).astype(BF16)


def f64(x):
    return np.asarray(x).astype(np.float64)


E2M1 = np.array([0.0, 0.5, 1.0, 1.5, 2.0, 3.0, 4.0, 6.0, -0.0, -0.5, -1.0, -1.5, -2.0, -3.0, -4.0, -6.0])


def pack_weight(w, fmt):
    k, n = w.shape
    w = f64(bf(w)).reshape(k // 32, 32, n)
    amax = np.abs(w).max(1)
    if fmt == "e4m3":
        byte = np.frexp(amax)[1] - 1 + 127 - 7
    else:
        mant, ex = np.frexp(amax / 6.0)
        byte = np.where(mant > 0.5, ex, ex - 1) + 127
    byte = np.clip(np.where(amax > 0, byte, 1), 1, 254)
    scaled = (w * np.exp2(127.0 - byte)[:, None, :]).reshape(k, n).astype(np.float32)
    by_word = np.ascontiguousarray(scaled.reshape(k // 512, 128, 4, n).transpose(0, 1, 3, 2))
    if fmt == "e4m3":
        words = by_word.astype(ml_dtypes.float8_e4m3fn).view(np.uint8)
    else:
        c = by_word.astype(ml_dtypes.float4_e2m1fn).view(np.uint8) & 0xF
        words = c[..., 0::2] | (c[..., 1::2] << 4)
    return np.ascontiguousarray(words), np.ascontiguousarray(byte.astype(np.uint8).reshape(k // 512, 16, n))


def unpack_weight(words, scales, fmt):
    g, p, n, _ = words.shape
    if fmt == "e4m3":
        vals = np.ascontiguousarray(words).view(ml_dtypes.float8_e4m3fn).astype(np.float64)
    else:
        nib = np.empty((g, p, n, 4), np.uint8)
        nib[..., 0::2] = words & 0xF
        nib[..., 1::2] = words >> 4
        vals = E2M1[nib]
    vals = vals * np.repeat(np.exp2(scales.astype(np.float64) - 127.0), 8, axis=1)[..., None]
    return vals.transpose(0, 1, 3, 2).reshape(g * 512, n)

def pack4(w):
    words, scales = pack_weight(w, "e2m1")
    return words.reshape(words.shape[0], 128, -1), scales


def unpack4(words, scales):
    return unpack_weight(words.reshape(words.shape[0], 128, -1, 2), scales, "e2m1")


B, I, C, K, L, S0, S1, S2, S3, S4 = 4, 32, 512, 7, 5, 16, 12, 8, 6, 4
P = S2 * S2


def setup_inputs():
    t = mx_kscale(C)
    q = bf(np.random.standard_normal((B, I, C)))
    feats = bf(np.random.standard_normal((B, C, S2, S2)) * t[:, None, None])
    po_w = np.random.standard_normal((C, C)) / np.sqrt(C) / t
    words, scales = pack4(np.ascontiguousarray(po_w.T))
    po_b = bf(np.random.standard_normal(C) * 0.3)
    return {"q": q,
            "feats": feats,
            "po_w_words": words,
            "po_w_scales": scales,
            "po_b": po_b}


def reference(q, feats, po_w_words, po_w_scales, po_b):
    m = f64(q)[:, :, :, None] * f64(feats).reshape(B, C, P)[:, None]
    o = (unpack4(po_w_words, po_w_scales).T @ mxq(m, 2, "e4m3")) + f64(po_b)[:, None]
    return o.reshape(B, I, C, S2, S2)

@@ -1,0 +1,125 @@
+from contextlib import ExitStack
+
+import concourse.mybir as mybir
+from concourse.masks import make_identity
+
+F32 = mybir.dt.float32
+BF16 = mybir.dt.bfloat16
+I32 = mybir.dt.int32
+U32 = mybir.dt.uint32
+U8 = mybir.dt.uint8
+FP8X4 = mybir.dt.float8_e4m3fn_x4
+FP4X4 = mybir.dt.float4_e2m1fn_x4
+
+P = 128
+PACK = 4
+B = 4
+I = 32
+C = 512
+X = 64
+O_TILES = C // P
+GROUP = 8
+COLS = GROUP * X
+
+FLOPS = 2 * C * C * B * I * X
+
+
+def tile_rpn_modulator_pb_kernel(tc, q, feats, po_w_words, po_w_scales, po_b, out):
+    nc = tc.nc
+    mult = mybir.AluOpType.mult
+    identity_fn = mybir.ActivationFunctionType.Identity
+
+    with ExitStack() as ctx:
+        consts = ctx.enter_context(tc.tile_pool(name="consts", bufs=1))
+        stage = ctx.enter_context(tc.tile_pool(name="stage", bufs=3))
+        results = ctx.enter_context(tc.tile_pool(name="results", bufs=16))
+        psum_head = ctx.enter_context(tc.psum_pool(name="psum_head", bufs=1))
+        psum_acc = ctx.enter_context(tc.psum_pool(name="psum_acc", bufs=6))
+
+        q_sb = consts.tile([P, C], BF16)
+        nc.sync.dma_start(out=q_sb[:], in_=q.rearrange("b i c -> (b i) c"))
+        f_raw = consts.tile([P, B, PACK, X], BF16)
+        nc.scalar.dma_start(
+            out=f_raw[:].rearrange("p b t x -> p b (t x)"),
+            in_=feats.rearrange("b (p t) y x -> p b (t y x)", t=PACK),
+        )
+        w_words = consts.tile([P, 2 * C], U8, align_bytes=64)
+        nc.sync.dma_start(out=w_words[:].bitcast(I32), in_=po_w_words[0].bitcast(I32))
+        w_scales = consts.tile([P, C], U8, align_bytes=64)
+        nc.vector.memset(w_scales[:].bitcast(I32), 0)
+        for quad in range(4):
+            nc.sync.dma_start(
+                out=w_scales[32 * quad : 32 * quad + 4, :].bitcast(I32),
+                in_=po_w_scales[0, 4 * quad : 4 * quad + 4, :].bitcast(I32),
+            )
+        bias_rows = consts.tile([O_TILES, P], BF16)
+        nc.scalar.dma_start(out=bias_rows[:], in_=po_b.rearrange("(j m) -> j m", j=O_TILES))
+
+        ident = consts.tile([P, P], F32)
+        make_identity(nc, ident[:])
+
+        q_pairs = q_sb[:].bitcast(F32)
+        qT_ps = psum_head.tile([P, 2, P], F32)
+        for u in range(2):
+            nc.tensor.transpose(qT_ps[:, u, :], q_pairs[:, u : C // 2 : 2], ident[:])
+        qT = consts.tile([P, B * I, PACK], BF16)
+        nc.vector.tensor_copy(
+            out=qT[:].rearrange("p r t -> p (r t)").bitcast(F32).rearrange("p (r u) -> p r u", u=2),
+            in_=qT_ps[:].rearrange("p u r -> p r u"),
+        )
+
+        f4 = consts.tile([P, B, X, PACK], BF16)
+        nc.vector.tensor_copy(out=f4[:], in_=f_raw[:].rearrange("p b t x -> p b x t"))
+
+        bias_sq = consts.tile([P, P], F32)
+        nc.vector.memset(bias_sq[:], 0.0)
+        nc.vector.tensor_copy(out=bias_sq[0:O_TILES, :], in_=bias_rows[:])
+        biasT_ps = psum_head.tile([P, P], F32)
+        nc.tensor.transpose(biasT_ps[:], bias_sq[:], ident[:])
+        bias_col = consts.tile([P, O_TILES], F32)
+        nc.vector.tensor_copy(out=bias_col[:], in_=biasT_ps[:, 0:O_TILES])
+
+        out_v = out.rearrange("b i (j m) y x -> b j m i (y x)", j=O_TILES)
+
+        for b in range(B):
+            for i0 in range(0, I, GROUP):
+                r0 = I * b + i0
+                m_bf = stage.tile([P, GROUP, X, PACK], BF16, align_bytes=64)
+                nc.vector.tensor_tensor(
+                    out=m_bf[:],
+                    in0=qT[:, r0 : r0 + GROUP, :].unsqueeze(2).to_broadcast([P, GROUP, X, PACK]),
+                    in1=f4[:, b].unsqueeze(1).to_broadcast([P, GROUP, X, PACK]),
+                    op=mult,
+                )
+                m_codes = stage.tile([P, COLS], U32, align_bytes=64)
+                m_scales = stage.tile([P, COLS], U8, align_bytes=64)
+                nc.vector.quantize_mx(
+                    out=m_codes[:].bitcast(FP8X4),
+                    scales=m_scales[:],
+                    in_=m_bf[:].rearrange("p i x t -> p (i x t)"),
+                )
+                o_sb = results.tile([P, O_TILES, COLS], F32)
+                for j in range(O_TILES):
+                    acc = psum_acc.tile([P, COLS], F32)
+                    nc.tensor.matmul_mx(
+                        out=acc[:],
+                        lhsT=w_words[:, 2 * P * j : 2 * P * (j + 1)].bitcast(FP4X4),
+                        lhsT_scale=w_scales[:, P * j : P * (j + 1)],
+                        rhs=m_codes[:].bitcast(FP8X4),
+                        rhs_scale=m_scales[:],
+                        start=True,
+                        stop=True,
+                    )
+                    if j < O_TILES - 1:
+                        nc.scalar.activation(
+                            out=o_sb[:, j, :], in_=acc[:], func=identity_fn,
+                            bias=bias_col[:, j : j + 1], scale=1.0,
+                        )
+                    else:
+                        nc.vector.tensor_scalar_add(
+                            out=o_sb[:, j, :], in0=acc[:], scalar1=bias_col[:, j : j + 1]
+                        )
+                    nc.sync.dma_start(
+                        out=out_v[b, j][:, i0 : i0 + GROUP, :],
+                        in_=o_sb[:, j, :].rearrange("p (i x) -> p i x", x=X),
+                    )

@@ -17,9 +17,11 @@ B = 4
 I = 32
 C = 512
 X = 64
-O_TILES = C // P
+O_PER_P = C // P
 GROUP = 8
 COLS = GROUP * X
+BLOCKS = COLS // P
+ROUNDS = B * I // GROUP
 
 FLOPS = 2 * C * C * B * I * X
 
@@ -30,11 +32,14 @@ def tile_rpn_modulator_pb_kernel(tc, q, feats, po_w_words, po_w_scales, po_b, ou
     identity_fn = mybir.ActivationFunctionType.Identity
 
     with ExitStack() as ctx:
+        ctx.enter_context(tc.manual_schedule())
         consts = ctx.enter_context(tc.tile_pool(name="consts", bufs=1))
-        stage = ctx.enter_context(tc.tile_pool(name="stage", bufs=3))
-        results = ctx.enter_context(tc.tile_pool(name="results", bufs=16))
-        psum_head = ctx.enter_context(tc.psum_pool(name="psum_head", bufs=1))
-        psum_acc = ctx.enter_context(tc.psum_pool(name="psum_acc", bufs=6))
+        m_pool = ctx.enter_context(tc.tile_pool(name="m_pool", bufs=3))
+        code_pool = ctx.enter_context(tc.tile_pool(name="code_pool", bufs=4))
+        prod_pool = ctx.enter_context(tc.tile_pool(name="prod_pool", bufs=2 * BLOCKS))
+        result_pool = ctx.enter_context(tc.tile_pool(name="result_pool", bufs=6))
+        prod_psum = ctx.enter_context(tc.psum_pool(name="prod_psum", bufs=BLOCKS))
+        turned_psum = ctx.enter_context(tc.psum_pool(name="turned_psum", bufs=O_PER_P))
 
         q_sb = consts.tile([P, C], BF16)
         nc.sync.dma_start(out=q_sb[:], in_=q.rearrange("b i c -> (b i) c"))
@@ -52,74 +57,111 @@ def tile_rpn_modulator_pb_kernel(tc, q, feats, po_w_words, po_w_scales, po_b, ou
                 out=w_scales[32 * quad : 32 * quad + 4, :].bitcast(I32),
                 in_=po_w_scales[0, 4 * quad : 4 * quad + 4, :].bitcast(I32),
             )
-        bias_rows = consts.tile([O_TILES, P], BF16)
-        nc.scalar.dma_start(out=bias_rows[:], in_=po_b.rearrange("(j m) -> j m", j=O_TILES))
+        bias_bf = consts.tile([P, O_PER_P], BF16)
+        nc.scalar.dma_start(out=bias_bf[:], in_=po_b.rearrange("(p j) -> p j", j=O_PER_P))
 
         ident = consts.tile([P, P], F32)
         make_identity(nc, ident[:])
 
         q_pairs = q_sb[:].bitcast(F32)
-        qT_ps = psum_head.tile([P, 2, P], F32)
+        qT_ps = turned_psum.tile([P, C], F32, name="turned")
         for u in range(2):
-            nc.tensor.transpose(qT_ps[:, u, :], q_pairs[:, u : C // 2 : 2], ident[:])
+            nc.tensor.transpose(qT_ps[:, P * u : P * (u + 1)], q_pairs[:, u : C // 2 : 2], ident[:])
         qT = consts.tile([P, B * I, PACK], BF16)
         nc.vector.tensor_copy(
             out=qT[:].rearrange("p r t -> p (r t)").bitcast(F32).rearrange("p (r u) -> p r u", u=2),
-            in_=qT_ps[:].rearrange("p u r -> p r u"),
+            in_=qT_ps[:, 0 : 2 * P].rearrange("p (u r) -> p r u", u=2),
         )
-
         f4 = consts.tile([P, B, X, PACK], BF16)
         nc.vector.tensor_copy(out=f4[:], in_=f_raw[:].rearrange("p b t x -> p b x t"))
+        bias = consts.tile([P, O_PER_P], F32)
+        nc.vector.tensor_copy(out=bias[:], in_=bias_bf[:])
 
-        bias_sq = consts.tile([P, P], F32)
-        nc.vector.memset(bias_sq[:], 0.0)
-        nc.vector.tensor_copy(out=bias_sq[0:O_TILES, :], in_=bias_rows[:])
-        biasT_ps = psum_head.tile([P, P], F32)
-        nc.tensor.transpose(biasT_ps[:], bias_sq[:], ident[:])
-        bias_col = consts.tile([P, O_TILES], F32)
-        nc.vector.tensor_copy(out=bias_col[:], in_=biasT_ps[:, 0:O_TILES])
+        out_v = out.rearrange("b i (p j) y x -> b p i (j y x)", j=O_PER_P)
 
-        out_v = out.rearrange("b i (j m) y x -> b j m i (y x)", j=O_TILES)
+        m_bf = {}
+        m_codes = {}
+        m_scales = {}
+        prod_ps = {}
+        prod_sb = {}
 
-        for b in range(B):
-            for i0 in range(0, I, GROUP):
-                r0 = I * b + i0
-                m_bf = stage.tile([P, GROUP, X, PACK], BF16, align_bytes=64)
-                nc.vector.tensor_tensor(
-                    out=m_bf[:],
-                    in0=qT[:, r0 : r0 + GROUP, :].unsqueeze(2).to_broadcast([P, GROUP, X, PACK]),
-                    in1=f4[:, b].unsqueeze(1).to_broadcast([P, GROUP, X, PACK]),
-                    op=mult,
+        def multiply(g):
+            r0 = GROUP * g
+            m_bf[g] = m_pool.tile([P, GROUP, X, PACK], BF16, name="m_bf", align_bytes=64)
+            nc.vector.tensor_tensor(
+                out=m_bf[g][:],
+                in0=qT[:, r0 : r0 + GROUP, :].unsqueeze(2).to_broadcast([P, GROUP, X, PACK]),
+                in1=f4[:, r0 // I].unsqueeze(1).to_broadcast([P, GROUP, X, PACK]),
+                op=mult,
+            )
+
+        def quantise(g):
+            m_codes[g] = code_pool.tile([P, COLS], U32, name="m_codes", align_bytes=64)
+            m_scales[g] = code_pool.tile([P, COLS], U8, name="m_scales", align_bytes=64)
+            nc.vector.quantize_mx(
+                out=m_codes[g][:].bitcast(FP8X4),
+                scales=m_scales[g][:],
+                in_=m_bf[g][:].rearrange("p i x t -> p (i x t)"),
+            )
+
+        def products(g):
+            for k in range(BLOCKS):
+                prod_ps[g, k] = prod_psum.tile([P, C], F32, name="prod_ps")
+                nc.tensor.matmul_mx(
+                    out=prod_ps[g, k][:],
+                    lhsT=m_codes[g][:, P * k : P * (k + 1)].bitcast(FP8X4),
+                    lhsT_scale=m_scales[g][:, P * k : P * (k + 1)],
+                    rhs=w_words[:].bitcast(FP4X4),
+                    rhs_scale=w_scales[:],
+                    start=True,
+                    stop=True,
                 )
-                m_codes = stage.tile([P, COLS], U32, align_bytes=64)
-                m_scales = stage.tile([P, COLS], U8, align_bytes=64)
-                nc.vector.quantize_mx(
-                    out=m_codes[:].bitcast(FP8X4),
-                    scales=m_scales[:],
-                    in_=m_bf[:].rearrange("p i x t -> p (i x t)"),
+
+        def products_to_sbuf(g):
+            for k in range(BLOCKS):
+                prod_sb[g, k] = prod_pool.tile([P, O_PER_P, P], F32, name="prod_sb")
+                sorted_read = prod_ps[g, k][:].rearrange("c (p j) -> c j p", j=O_PER_P)
+                if k % 2 == 0:
+                    nc.vector.tensor_copy(out=prod_sb[g, k][:], in_=sorted_read)
+                else:
+                    nc.scalar.copy(out=prod_sb[g, k][:], in_=sorted_read)
+
+        def turn_and_store(g):
+            turned = []
+            for j in range(O_PER_P):
+                turned.append(turned_psum.tile([P, COLS], F32, name="turned"))
+                for k in range(BLOCKS):
+                    nc.tensor.transpose(
+                        turned[j][:, P * k : P * (k + 1)], prod_sb[g, k][:, j, :], ident[:]
+                    )
+            result = result_pool.tile([P, GROUP, O_PER_P, X], F32, name="result")
+            for j in range(O_PER_P):
+                nc.scalar.activation(
+                    out=result[:, :, j, :],
+                    in_=turned[j][:].rearrange("p (i x) -> p i x", x=X),
+                    func=identity_fn,
+                    bias=bias[:, j : j + 1],
+                    scale=1.0,
                 )
-                o_sb = results.tile([P, O_TILES, COLS], F32)
-                for j in range(O_TILES):
-                    acc = psum_acc.tile([P, COLS], F32)
-                    nc.tensor.matmul_mx(
-                        out=acc[:],
-                        lhsT=w_words[:, 2 * P * j : 2 * P * (j + 1)].bitcast(FP4X4),
-                        lhsT_scale=w_scales[:, P * j : P * (j + 1)],
-                        rhs=m_codes[:].bitcast(FP8X4),
-                        rhs_scale=m_scales[:],
-                        start=True,
-                        stop=True,
-                    )
-                    if j < O_TILES - 1:
-                        nc.scalar.activation(
-                            out=o_sb[:, j, :], in_=acc[:], func=identity_fn,
-                            bias=bias_col[:, j : j + 1], scale=1.0,
-                        )
-                    else:
-                        nc.vector.tensor_scalar_add(
-                            out=o_sb[:, j, :], in0=acc[:], scalar1=bias_col[:, j : j + 1]
-                        )
-                    nc.sync.dma_start(
-                        out=out_v[b, j][:, i0 : i0 + GROUP, :],
-                        in_=o_sb[:, j, :].rearrange("p (i x) -> p i x", x=X),
-                    )
+            i0 = (GROUP * g) % I
+            nc.sync.dma_start(
+                out=out_v[(GROUP * g) // I][:, i0 : i0 + GROUP, :],
+                in_=result[:].rearrange("p i j x -> p i (j x)"),
+            )
+
+        multiply(0)
+        quantise(0)
+        products(0)
+        multiply(1)
+        quantise(1)
+        products_to_sbuf(0)
+        multiply(2)
+        for g in range(ROUNDS):
+            if g + 1 < ROUNDS:
+                products(g + 1)
+                products_to_sbuf(g + 1)
+            if g + 2 < ROUNDS:
+                quantise(g + 2)
+            if g + 3 < ROUNDS:
+                multiply(g + 3)
+            turn_and_store(g)

@@ -73,7 +73,7 @@ def tile_rpn_modulator_pb_kernel(tc, q, feats, po_w_words, po_w_scales, po_b, ou
             in_=qT_ps[:, 0 : 2 * P].rearrange("p (u r) -> p r u", u=2),
         )
         f4 = consts.tile([P, B, X, PACK], BF16)
-        nc.vector.tensor_copy(out=f4[:], in_=f_raw[:].rearrange("p b t x -> p b x t"))
+        nc.scalar.copy(out=f4[:], in_=f_raw[:].rearrange("p b t x -> p b x t"))
         bias = consts.tile([P, O_PER_P], F32)
         nc.vector.tensor_copy(out=bias[:], in_=bias_bf[:])
 
@@ -136,13 +136,16 @@ def tile_rpn_modulator_pb_kernel(tc, q, feats, po_w_words, po_w_scales, po_b, ou
                     )
             result = result_pool.tile([P, GROUP, O_PER_P, X], F32, name="result")
             for j in range(O_PER_P):
-                nc.scalar.activation(
-                    out=result[:, :, j, :],
-                    in_=turned[j][:].rearrange("p (i x) -> p i x", x=X),
-                    func=identity_fn,
-                    bias=bias[:, j : j + 1],
-                    scale=1.0,
-                )
+                turned_view = turned[j][:].rearrange("p (i x) -> p i x", x=X)
+                if j == O_PER_P - 1 and g % 2 == 1:
+                    nc.vector.tensor_scalar_add(
+                        out=result[:, :, j, :], in0=turned_view, scalar1=bias[:, j : j + 1]
+                    )
+                else:
+                    nc.scalar.activation(
+                        out=result[:, :, j, :], in_=turned_view, func=identity_fn,
+                        bias=bias[:, j : j + 1], scale=1.0,
+                    )
             i0 = (GROUP * g) % I
             nc.sync.dma_start(
                 out=out_v[(GROUP * g) // I][:, i0 : i0 + GROUP, :],

@@ -20,8 +20,12 @@ X = 64
 O_PER_P = C // P
 GROUP = 8
 COLS = GROUP * X
-BLOCKS = COLS // P
-ROUNDS = B * I // GROUP
+BLOCK = P // X
+BLOCKS = GROUP // BLOCK
+TAPER = (2, 2, 4)
+ROUND_SIZES = TAPER + (GROUP,) * ((B * I - 2 * sum(TAPER)) // GROUP) + tuple(reversed(TAPER))
+ROUND_STARTS = tuple(sum(ROUND_SIZES[:g]) for g in range(len(ROUND_SIZES)))
+ROUNDS = len(ROUND_SIZES)
 
 FLOPS = 2 * C * C * B * I * X
 
@@ -86,26 +90,27 @@ def tile_rpn_modulator_pb_kernel(tc, q, feats, po_w_words, po_w_scales, po_b, ou
         prod_sb = {}
 
         def multiply(g):
-            r0 = GROUP * g
+            r0, n = ROUND_STARTS[g], ROUND_SIZES[g]
             m_bf[g] = m_pool.tile([P, GROUP, X, PACK], BF16, name="m_bf", align_bytes=64)
             nc.vector.tensor_tensor(
-                out=m_bf[g][:],
-                in0=qT[:, r0 : r0 + GROUP, :].unsqueeze(2).to_broadcast([P, GROUP, X, PACK]),
-                in1=f4[:, r0 // I].unsqueeze(1).to_broadcast([P, GROUP, X, PACK]),
+                out=m_bf[g][:, 0:n],
+                in0=qT[:, r0 : r0 + n, :].unsqueeze(2).to_broadcast([P, n, X, PACK]),
+                in1=f4[:, r0 // I].unsqueeze(1).to_broadcast([P, n, X, PACK]),
                 op=mult,
             )
 
         def quantise(g):
             m_codes[g] = code_pool.tile([P, COLS], U32, name="m_codes", align_bytes=64)
             m_scales[g] = code_pool.tile([P, COLS], U8, name="m_scales", align_bytes=64)
+            cols = ROUND_SIZES[g] * X
             nc.vector.quantize_mx(
-                out=m_codes[g][:].bitcast(FP8X4),
-                scales=m_scales[g][:],
-                in_=m_bf[g][:].rearrange("p i x t -> p (i x t)"),
+                out=m_codes[g][:, 0:cols].bitcast(FP8X4),
+                scales=m_scales[g][:, 0:cols],
+                in_=m_bf[g][:, 0 : ROUND_SIZES[g]].rearrange("p i x t -> p (i x t)"),
             )
 
         def products(g):
-            for k in range(BLOCKS):
+            for k in range(ROUND_SIZES[g] // BLOCK):
                 prod_ps[g, k] = prod_psum.tile([P, C], F32, name="prod_ps")
                 nc.tensor.matmul_mx(
                     out=prod_ps[g, k][:],
@@ -118,38 +123,38 @@ def tile_rpn_modulator_pb_kernel(tc, q, feats, po_w_words, po_w_scales, po_b, ou
                 )
 
         def products_to_sbuf(g):
-            for k in range(BLOCKS):
+            for k in range(ROUND_SIZES[g] // BLOCK):
                 prod_sb[g, k] = prod_pool.tile([P, O_PER_P, P], F32, name="prod_sb")
                 sorted_read = prod_ps[g, k][:].rearrange("c (p j) -> c j p", j=O_PER_P)
                 if k % 2 == 0:
-                    nc.vector.tensor_copy(out=prod_sb[g, k][:], in_=sorted_read)
-                else:
                     nc.scalar.copy(out=prod_sb[g, k][:], in_=sorted_read)
+                else:
+                    nc.vector.tensor_copy(out=prod_sb[g, k][:], in_=sorted_read)
 
         def turn_and_store(g):
+            r0, n = ROUND_STARTS[g], ROUND_SIZES[g]
             turned = []
             for j in range(O_PER_P):
                 turned.append(turned_psum.tile([P, COLS], F32, name="turned"))
-                for k in range(BLOCKS):
+                for k in range(n // BLOCK):
                     nc.tensor.transpose(
                         turned[j][:, P * k : P * (k + 1)], prod_sb[g, k][:, j, :], ident[:]
                     )
             result = result_pool.tile([P, GROUP, O_PER_P, X], F32, name="result")
             for j in range(O_PER_P):
-                turned_view = turned[j][:].rearrange("p (i x) -> p i x", x=X)
+                turned_view = turned[j][:, 0 : n * X].rearrange("p (i x) -> p i x", x=X)
                 if j == O_PER_P - 1 and g % 2 == 1:
                     nc.vector.tensor_scalar_add(
-                        out=result[:, :, j, :], in0=turned_view, scalar1=bias[:, j : j + 1]
+                        out=result[:, 0:n, j, :], in0=turned_view, scalar1=bias[:, j : j + 1]
                     )
                 else:
                     nc.scalar.activation(
-                        out=result[:, :, j, :], in_=turned_view, func=identity_fn,
+                        out=result[:, 0:n, j, :], in_=turned_view, func=identity_fn,
                         bias=bias[:, j : j + 1], scale=1.0,
                     )
-            i0 = (GROUP * g) % I
             nc.sync.dma_start(
-                out=out_v[(GROUP * g) // I][:, i0 : i0 + GROUP, :],
-                in_=result[:].rearrange("p i j x -> p i (j x)"),
+                out=out_v[r0 // I][:, r0 % I : r0 % I + n, :],
+                in_=result[:, 0:n].rearrange("p i j x -> p i (j x)"),
             )
 
         multiply(0)

@@ -20,12 +20,9 @@ X = 64
 O_PER_P = C // P
 GROUP = 8
 COLS = GROUP * X
-BLOCK = P // X
-BLOCKS = GROUP // BLOCK
-TAPER = (2, 2, 4)
-ROUND_SIZES = TAPER + (GROUP,) * ((B * I - 2 * sum(TAPER)) // GROUP) + tuple(reversed(TAPER))
-ROUND_STARTS = tuple(sum(ROUND_SIZES[:g]) for g in range(len(ROUND_SIZES)))
-ROUNDS = len(ROUND_SIZES)
+BLOCKS = COLS // P
+ROUNDS = B * I // GROUP
+GPSIMD_SHARE = 2
 
 FLOPS = 2 * C * C * B * I * X
 
@@ -90,27 +87,30 @@ def tile_rpn_modulator_pb_kernel(tc, q, feats, po_w_words, po_w_scales, po_b, ou
         prod_sb = {}
 
         def multiply(g):
-            r0, n = ROUND_STARTS[g], ROUND_SIZES[g]
+            r0 = GROUP * g
             m_bf[g] = m_pool.tile([P, GROUP, X, PACK], BF16, name="m_bf", align_bytes=64)
-            nc.vector.tensor_tensor(
-                out=m_bf[g][:, 0:n],
-                in0=qT[:, r0 : r0 + n, :].unsqueeze(2).to_broadcast([P, n, X, PACK]),
-                in1=f4[:, r0 // I].unsqueeze(1).to_broadcast([P, n, X, PACK]),
-                op=mult,
-            )
+            split = GROUP - GPSIMD_SHARE
+            for engine, first, count in ((nc.vector, 0, split), (nc.gpsimd, split, GPSIMD_SHARE)):
+                engine.tensor_tensor(
+                    out=m_bf[g][:, first : first + count],
+                    in0=qT[:, r0 + first : r0 + first + count, :]
+                    .unsqueeze(2)
+                    .to_broadcast([P, count, X, PACK]),
+                    in1=f4[:, r0 // I].unsqueeze(1).to_broadcast([P, count, X, PACK]),
+                    op=mult,
+                )
 
         def quantise(g):
             m_codes[g] = code_pool.tile([P, COLS], U32, name="m_codes", align_bytes=64)
             m_scales[g] = code_pool.tile([P, COLS], U8, name="m_scales", align_bytes=64)
-            cols = ROUND_SIZES[g] * X
             nc.vector.quantize_mx(
-                out=m_codes[g][:, 0:cols].bitcast(FP8X4),
-                scales=m_scales[g][:, 0:cols],
-                in_=m_bf[g][:, 0 : ROUND_SIZES[g]].rearrange("p i x t -> p (i x t)"),
+                out=m_codes[g][:].bitcast(FP8X4),
+                scales=m_scales[g][:],
+                in_=m_bf[g][:].rearrange("p i x t -> p (i x t)"),
             )
 
         def products(g):
-            for k in range(ROUND_SIZES[g] // BLOCK):
+            for k in range(BLOCKS):
                 prod_ps[g, k] = prod_psum.tile([P, C], F32, name="prod_ps")
                 nc.tensor.matmul_mx(
                     out=prod_ps[g, k][:],
@@ -123,38 +123,38 @@ def tile_rpn_modulator_pb_kernel(tc, q, feats, po_w_words, po_w_scales, po_b, ou
                 )
 
         def products_to_sbuf(g):
-            for k in range(ROUND_SIZES[g] // BLOCK):
+            for k in range(BLOCKS):
                 prod_sb[g, k] = prod_pool.tile([P, O_PER_P, P], F32, name="prod_sb")
                 sorted_read = prod_ps[g, k][:].rearrange("c (p j) -> c j p", j=O_PER_P)
                 if k % 2 == 0:
-                    nc.scalar.copy(out=prod_sb[g, k][:], in_=sorted_read)
-                else:
                     nc.vector.tensor_copy(out=prod_sb[g, k][:], in_=sorted_read)
+                else:
+                    nc.scalar.copy(out=prod_sb[g, k][:], in_=sorted_read)
 
         def turn_and_store(g):
-            r0, n = ROUND_STARTS[g], ROUND_SIZES[g]
             turned = []
             for j in range(O_PER_P):
                 turned.append(turned_psum.tile([P, COLS], F32, name="turned"))
-                for k in range(n // BLOCK):
+                for k in range(BLOCKS):
                     nc.tensor.transpose(
                         turned[j][:, P * k : P * (k + 1)], prod_sb[g, k][:, j, :], ident[:]
                     )
             result = result_pool.tile([P, GROUP, O_PER_P, X], F32, name="result")
             for j in range(O_PER_P):
-                turned_view = turned[j][:, 0 : n * X].rearrange("p (i x) -> p i x", x=X)
-                if j == O_PER_P - 1 and g % 2 == 1:
+                turned_view = turned[j][:].rearrange("p (i x) -> p i x", x=X)
+                if j == O_PER_P - 1 and g % 4 != 0:
                     nc.vector.tensor_scalar_add(
-                        out=result[:, 0:n, j, :], in0=turned_view, scalar1=bias[:, j : j + 1]
+                        out=result[:, :, j, :], in0=turned_view, scalar1=bias[:, j : j + 1]
                     )
                 else:
                     nc.scalar.activation(
-                        out=result[:, 0:n, j, :], in_=turned_view, func=identity_fn,
+                        out=result[:, :, j, :], in_=turned_view, func=identity_fn,
                         bias=bias[:, j : j + 1], scale=1.0,
                     )
+            i0 = (GROUP * g) % I
             nc.sync.dma_start(
-                out=out_v[r0 // I][:, r0 % I : r0 % I + n, :],
-                in_=result[:, 0:n].rearrange("p i j x -> p i (j x)"),
+                out=out_v[(GROUP * g) // I][:, i0 : i0 + GROUP, :],
+                in_=result[:].rearrange("p i j x -> p i (j x)"),
             )
 
         multiply(0)

@@ -20,9 +20,8 @@ X = 64
 O_PER_P = C // P
 GROUP = 8
 COLS = GROUP * X
-BLOCKS = COLS // P
 ROUNDS = B * I // GROUP
-GPSIMD_SHARE = 2
+WORD_BYTES = 2
 
 FLOPS = 2 * C * C * B * I * X
 
@@ -37,11 +36,11 @@ def tile_rpn_modulator_pb_kernel(tc, q, feats, po_w_words, po_w_scales, po_b, ou
         consts = ctx.enter_context(tc.tile_pool(name="consts", bufs=1))
         m_pool = ctx.enter_context(tc.tile_pool(name="m_pool", bufs=3))
         code_pool = ctx.enter_context(tc.tile_pool(name="code_pool", bufs=4))
-        prod_pool = ctx.enter_context(tc.tile_pool(name="prod_pool", bufs=2 * BLOCKS))
-        result_pool = ctx.enter_context(tc.tile_pool(name="result_pool", bufs=6))
-        prod_psum = ctx.enter_context(tc.psum_pool(name="prod_psum", bufs=BLOCKS))
-        turned_psum = ctx.enter_context(tc.psum_pool(name="turned_psum", bufs=O_PER_P))
+        result_pool = ctx.enter_context(tc.tile_pool(name="result_pool", bufs=4))
+        psum = ctx.enter_context(tc.psum_pool(name="psum", bufs=2 * O_PER_P))
 
+        scales_raw = consts.tile([P, C], U8, align_bytes=64)
+        nc.vector.memset(scales_raw[:].bitcast(I32), 0)
         q_sb = consts.tile([P, C], BF16)
         nc.sync.dma_start(out=q_sb[:], in_=q.rearrange("b i c -> (b i) c"))
         f_raw = consts.tile([P, B, PACK, X], BF16)
@@ -49,13 +48,11 @@ def tile_rpn_modulator_pb_kernel(tc, q, feats, po_w_words, po_w_scales, po_b, ou
             out=f_raw[:].rearrange("p b t x -> p b (t x)"),
             in_=feats.rearrange("b (p t) y x -> p b (t y x)", t=PACK),
         )
-        w_words = consts.tile([P, 2 * C], U8, align_bytes=64)
-        nc.sync.dma_start(out=w_words[:].bitcast(I32), in_=po_w_words[0].bitcast(I32))
-        w_scales = consts.tile([P, C], U8, align_bytes=64)
-        nc.vector.memset(w_scales[:].bitcast(I32), 0)
+        words_raw = consts.tile([P, WORD_BYTES * C], U8, align_bytes=64)
+        nc.sync.dma_start(out=words_raw[:].bitcast(I32), in_=po_w_words[0].bitcast(I32))
         for quad in range(4):
             nc.sync.dma_start(
-                out=w_scales[32 * quad : 32 * quad + 4, :].bitcast(I32),
+                out=scales_raw[32 * quad : 32 * quad + 4, :].bitcast(I32),
                 in_=po_w_scales[0, 4 * quad : 4 * quad + 4, :].bitcast(I32),
             )
         bias_bf = consts.tile([P, O_PER_P], BF16)
@@ -63,9 +60,11 @@ def tile_rpn_modulator_pb_kernel(tc, q, feats, po_w_words, po_w_scales, po_b, ou
 
         ident = consts.tile([P, P], F32)
         make_identity(nc, ident[:])
+        bias = consts.tile([P, O_PER_P], F32)
+        nc.gpsimd.tensor_copy(out=bias[:], in_=bias_bf[:])
 
         q_pairs = q_sb[:].bitcast(F32)
-        qT_ps = turned_psum.tile([P, C], F32, name="turned")
+        qT_ps = psum.tile([P, COLS], F32, name="acc")
         for u in range(2):
             nc.tensor.transpose(qT_ps[:, P * u : P * (u + 1)], q_pairs[:, u : C // 2 : 2], ident[:])
         qT = consts.tile([P, B * I, PACK], BF16)
@@ -74,31 +73,25 @@ def tile_rpn_modulator_pb_kernel(tc, q, feats, po_w_words, po_w_scales, po_b, ou
             in_=qT_ps[:, 0 : 2 * P].rearrange("p (u r) -> p r u", u=2),
         )
         f4 = consts.tile([P, B, X, PACK], BF16)
-        nc.scalar.copy(out=f4[:], in_=f_raw[:].rearrange("p b t x -> p b x t"))
-        bias = consts.tile([P, O_PER_P], F32)
-        nc.vector.tensor_copy(out=bias[:], in_=bias_bf[:])
+        for b in range(B):
+            nc.scalar.copy(out=f4[:, b], in_=f_raw[:, b].rearrange("p t x -> p x t"))
 
         out_v = out.rearrange("b i (p j) y x -> b p i (j y x)", j=O_PER_P)
 
         m_bf = {}
         m_codes = {}
         m_scales = {}
-        prod_ps = {}
-        prod_sb = {}
+        acc = {}
 
         def multiply(g):
             r0 = GROUP * g
             m_bf[g] = m_pool.tile([P, GROUP, X, PACK], BF16, name="m_bf", align_bytes=64)
-            split = GROUP - GPSIMD_SHARE
-            for engine, first, count in ((nc.vector, 0, split), (nc.gpsimd, split, GPSIMD_SHARE)):
-                engine.tensor_tensor(
-                    out=m_bf[g][:, first : first + count],
-                    in0=qT[:, r0 + first : r0 + first + count, :]
-                    .unsqueeze(2)
-                    .to_broadcast([P, count, X, PACK]),
-                    in1=f4[:, r0 // I].unsqueeze(1).to_broadcast([P, count, X, PACK]),
-                    op=mult,
-                )
+            nc.vector.tensor_tensor(
+                out=m_bf[g][:],
+                in0=qT[:, r0 : r0 + GROUP, :].unsqueeze(2).to_broadcast([P, GROUP, X, PACK]),
+                in1=f4[:, r0 // I].unsqueeze(1).to_broadcast([P, GROUP, X, PACK]),
+                op=mult,
+            )
 
         def quantise(g):
             m_codes[g] = code_pool.tile([P, COLS], U32, name="m_codes", align_bytes=64)
@@ -110,45 +103,29 @@ def tile_rpn_modulator_pb_kernel(tc, q, feats, po_w_words, po_w_scales, po_b, ou
             )
 
         def products(g):
-            for k in range(BLOCKS):
-                prod_ps[g, k] = prod_psum.tile([P, C], F32, name="prod_ps")
+            for j in range(O_PER_P):
+                acc[g, j] = psum.tile([P, COLS], F32, name="acc")
                 nc.tensor.matmul_mx(
-                    out=prod_ps[g, k][:],
-                    lhsT=m_codes[g][:, P * k : P * (k + 1)].bitcast(FP8X4),
-                    lhsT_scale=m_scales[g][:, P * k : P * (k + 1)],
-                    rhs=w_words[:].bitcast(FP4X4),
-                    rhs_scale=w_scales[:],
+                    out=acc[g, j][:],
+                    lhsT=words[:, WORD_BYTES * P * j : WORD_BYTES * P * (j + 1)].bitcast(FP4X4),
+                    lhsT_scale=scales[:, P * j : P * (j + 1)],
+                    rhs=m_codes[g][:].bitcast(FP8X4),
+                    rhs_scale=m_scales[g][:],
                     start=True,
                     stop=True,
                 )
 
-        def products_to_sbuf(g):
-            for k in range(BLOCKS):
-                prod_sb[g, k] = prod_pool.tile([P, O_PER_P, P], F32, name="prod_sb")
-                sorted_read = prod_ps[g, k][:].rearrange("c (p j) -> c j p", j=O_PER_P)
-                if k % 2 == 0:
-                    nc.vector.tensor_copy(out=prod_sb[g, k][:], in_=sorted_read)
-                else:
-                    nc.scalar.copy(out=prod_sb[g, k][:], in_=sorted_read)
-
-        def turn_and_store(g):
-            turned = []
-            for j in range(O_PER_P):
-                turned.append(turned_psum.tile([P, COLS], F32, name="turned"))
-                for k in range(BLOCKS):
-                    nc.tensor.transpose(
-                        turned[j][:, P * k : P * (k + 1)], prod_sb[g, k][:, j, :], ident[:]
-                    )
+        def empty_and_store(g):
             result = result_pool.tile([P, GROUP, O_PER_P, X], F32, name="result")
             for j in range(O_PER_P):
-                turned_view = turned[j][:].rearrange("p (i x) -> p i x", x=X)
-                if j == O_PER_P - 1 and g % 4 != 0:
+                bank = acc[g, j][:].rearrange("p (i x) -> p i x", x=X)
+                if j == O_PER_P - 1 and g % 2 == 1:
                     nc.vector.tensor_scalar_add(
-                        out=result[:, :, j, :], in0=turned_view, scalar1=bias[:, j : j + 1]
+                        out=result[:, :, j, :], in0=bank, scalar1=bias[:, j : j + 1]
                     )
                 else:
                     nc.scalar.activation(
-                        out=result[:, :, j, :], in_=turned_view, func=identity_fn,
+                        out=result[:, :, j, :], in_=bank, func=identity_fn,
                         bias=bias[:, j : j + 1], scale=1.0,
                     )
             i0 = (GROUP * g) % I
@@ -158,18 +135,26 @@ def tile_rpn_modulator_pb_kernel(tc, q, feats, po_w_words, po_w_scales, po_b, ou
             )
 
         multiply(0)
+        words = consts.tile([P, WORD_BYTES * C], U8, align_bytes=64)
+        nc.vector.tensor_copy(
+            out=words[:].rearrange("p (j n e) -> p n j e", j=O_PER_P, e=WORD_BYTES),
+            in_=words_raw[:].rearrange("p (n j e) -> p n j e", j=O_PER_P, e=WORD_BYTES),
+        )
+        scales = consts.tile([P, C], U8, align_bytes=64)
+        nc.vector.tensor_copy(
+            out=scales[:].rearrange("p (j n) -> p n j", j=O_PER_P),
+            in_=scales_raw[:].rearrange("p (n j) -> p n j", j=O_PER_P),
+        )
         quantise(0)
-        products(0)
         multiply(1)
+        products(0)
         quantise(1)
-        products_to_sbuf(0)
         multiply(2)
         for g in range(ROUNDS):
             if g + 1 < ROUNDS:
                 products(g + 1)
-                products_to_sbuf(g + 1)
             if g + 2 < ROUNDS:
                 quantise(g + 2)
             if g + 3 < ROUNDS:
                 multiply(g + 3)
-            turn_and_store(g)
+            empty_and_store(g)

@@ -119,15 +119,10 @@ def tile_rpn_modulator_pb_kernel(tc, q, feats, po_w_words, po_w_scales, po_b, ou
             result = result_pool.tile([P, GROUP, O_PER_P, X], F32, name="result")
             for j in range(O_PER_P):
                 bank = acc[g, j][:].rearrange("p (i x) -> p i x", x=X)
-                if j == O_PER_P - 1 and g % 2 == 1:
-                    nc.vector.tensor_scalar_add(
-                        out=result[:, :, j, :], in0=bank, scalar1=bias[:, j : j + 1]
-                    )
-                else:
-                    nc.scalar.activation(
-                        out=result[:, :, j, :], in_=bank, func=identity_fn,
-                        bias=bias[:, j : j + 1], scale=1.0,
-                    )
+                nc.scalar.activation(
+                    out=result[:, :, j, :], in_=bank, func=identity_fn,
+                    bias=bias[:, j : j + 1], scale=1.0,
+                )
             i0 = (GROUP * g) % I
             nc.sync.dma_start(
                 out=out_v[(GROUP * g) // I][:, i0 : i0 + GROUP, :],

@@ -20,7 +20,9 @@ X = 64
 O_PER_P = C // P
 GROUP = 8
 COLS = GROUP * X
-ROUNDS = B * I // GROUP
+SIZES = [4, 4] + [GROUP] * ((B * I - GROUP) // GROUP)
+STARTS = [sum(SIZES[:g]) for g in range(len(SIZES))]
+ROUNDS = len(SIZES)
 WORD_BYTES = 2
 
 FLOPS = 2 * C * C * B * I * X
@@ -41,27 +43,49 @@ def tile_rpn_modulator_pb_kernel(tc, q, feats, po_w_words, po_w_scales, po_b, ou
 
         scales_raw = consts.tile([P, C], U8, align_bytes=64)
         nc.vector.memset(scales_raw[:].bitcast(I32), 0)
-        q_sb = consts.tile([P, C], BF16)
-        nc.sync.dma_start(out=q_sb[:], in_=q.rearrange("b i c -> (b i) c"))
-        f_raw = consts.tile([P, B, PACK, X], BF16)
-        nc.scalar.dma_start(
-            out=f_raw[:].rearrange("p b t x -> p b (t x)"),
-            in_=feats.rearrange("b (p t) y x -> p b (t y x)", t=PACK),
-        )
         words_raw = consts.tile([P, WORD_BYTES * C], U8, align_bytes=64)
         nc.sync.dma_start(out=words_raw[:].bitcast(I32), in_=po_w_words[0].bitcast(I32))
+        q_sb = consts.tile([P, C], BF16)
+        nc.scalar.dma_start(out=q_sb[:], in_=q.rearrange("b i c -> (b i) c"))
+        f_raw = consts.tile([P, B, PACK, X], BF16)
+        nc.sync.dma_start(
+            out=f_raw[:, 0].rearrange("p t x -> p (t x)"),
+            in_=feats[0].rearrange("(p t) y x -> p (t y x)", t=PACK),
+        )
         for quad in range(4):
             nc.sync.dma_start(
                 out=scales_raw[32 * quad : 32 * quad + 4, :].bitcast(I32),
                 in_=po_w_scales[0, 4 * quad : 4 * quad + 4, :].bitcast(I32),
             )
+        nc.scalar.dma_start(
+            out=f_raw[:, 1:B].rearrange("p b t x -> p b (t x)"),
+            in_=feats[1:B].rearrange("b (p t) y x -> p b (t y x)", t=PACK),
+        )
         bias_bf = consts.tile([P, O_PER_P], BF16)
         nc.scalar.dma_start(out=bias_bf[:], in_=po_b.rearrange("(p j) -> p j", j=O_PER_P))
+
+        warm = consts.tile([P, 2], F32)
+        nc.vector.memset(warm[:], 0.0)
+        nc.scalar.activation(out=warm[:, 1:2], in_=warm[:, 0:1], func=identity_fn, scale=1.0)
 
         ident = consts.tile([P, P], F32)
         make_identity(nc, ident[:])
         bias = consts.tile([P, O_PER_P], F32)
         nc.gpsimd.tensor_copy(out=bias[:], in_=bias_bf[:])
+
+        words = consts.tile([P, WORD_BYTES * C], U8, align_bytes=64)
+        scales = consts.tile([P, C], U8, align_bytes=64)
+
+        def sort_words(j0, j1):
+            nc.vector.tensor_copy(
+                out=words[:, WORD_BYTES * P * j0 : WORD_BYTES * P * j1].rearrange(
+                    "p (j n e) -> p j n e", j=j1 - j0, e=WORD_BYTES
+                ),
+                in_=words_raw[:].rearrange("p (n j e) -> p j n e", j=O_PER_P, e=WORD_BYTES)[:, j0:j1],
+            )
+
+        sort_words(0, 2)
+        sort_words(2, 4)
 
         q_pairs = q_sb[:].bitcast(F32)
         qT_ps = psum.tile([P, COLS], F32, name="acc")
@@ -84,61 +108,57 @@ def tile_rpn_modulator_pb_kernel(tc, q, feats, po_w_words, po_w_scales, po_b, ou
         acc = {}
 
         def multiply(g):
-            r0 = GROUP * g
+            r0, n = STARTS[g], SIZES[g]
             m_bf[g] = m_pool.tile([P, GROUP, X, PACK], BF16, name="m_bf", align_bytes=64)
             nc.vector.tensor_tensor(
-                out=m_bf[g][:],
-                in0=qT[:, r0 : r0 + GROUP, :].unsqueeze(2).to_broadcast([P, GROUP, X, PACK]),
-                in1=f4[:, r0 // I].unsqueeze(1).to_broadcast([P, GROUP, X, PACK]),
+                out=m_bf[g][:, 0:n],
+                in0=qT[:, r0 : r0 + n, :].unsqueeze(2).to_broadcast([P, n, X, PACK]),
+                in1=f4[:, r0 // I].unsqueeze(1).to_broadcast([P, n, X, PACK]),
                 op=mult,
             )
 
         def quantise(g):
             m_codes[g] = code_pool.tile([P, COLS], U32, name="m_codes", align_bytes=64)
             m_scales[g] = code_pool.tile([P, COLS], U8, name="m_scales", align_bytes=64)
+            cols = X * SIZES[g]
             nc.vector.quantize_mx(
-                out=m_codes[g][:].bitcast(FP8X4),
-                scales=m_scales[g][:],
-                in_=m_bf[g][:].rearrange("p i x t -> p (i x t)"),
+                out=m_codes[g][:, 0:cols].bitcast(FP8X4),
+                scales=m_scales[g][:, 0:cols],
+                in_=m_bf[g][:, 0 : SIZES[g]].rearrange("p i x t -> p (i x t)"),
             )
 
         def products(g):
+            cols = X * SIZES[g]
             for j in range(O_PER_P):
                 acc[g, j] = psum.tile([P, COLS], F32, name="acc")
                 nc.tensor.matmul_mx(
-                    out=acc[g, j][:],
+                    out=acc[g, j][:, 0:cols],
                     lhsT=words[:, WORD_BYTES * P * j : WORD_BYTES * P * (j + 1)].bitcast(FP4X4),
                     lhsT_scale=scales[:, P * j : P * (j + 1)],
-                    rhs=m_codes[g][:].bitcast(FP8X4),
-                    rhs_scale=m_scales[g][:],
+                    rhs=m_codes[g][:, 0:cols].bitcast(FP8X4),
+                    rhs_scale=m_scales[g][:, 0:cols],
                     start=True,
                     stop=True,
                 )
 
         def empty_and_store(g):
+            r0, n = STARTS[g], SIZES[g]
             result = result_pool.tile([P, GROUP, O_PER_P, X], F32, name="result")
             for j in range(O_PER_P):
-                bank = acc[g, j][:].rearrange("p (i x) -> p i x", x=X)
+                bank = acc[g, j][:, 0 : X * n].rearrange("p (i x) -> p i x", x=X)
                 nc.scalar.activation(
-                    out=result[:, :, j, :], in_=bank, func=identity_fn,
+                    out=result[:, 0:n, j, :], in_=bank, func=identity_fn,
                     bias=bias[:, j : j + 1], scale=1.0,
                 )
-            i0 = (GROUP * g) % I
             nc.sync.dma_start(
-                out=out_v[(GROUP * g) // I][:, i0 : i0 + GROUP, :],
-                in_=result[:].rearrange("p i j x -> p i (j x)"),
+                out=out_v[r0 // I][:, r0 % I : r0 % I + n, :],
+                in_=result[:, 0:n].rearrange("p i j x -> p i (j x)"),
             )
 
         multiply(0)
-        words = consts.tile([P, WORD_BYTES * C], U8, align_bytes=64)
         nc.vector.tensor_copy(
-            out=words[:].rearrange("p (j n e) -> p n j e", j=O_PER_P, e=WORD_BYTES),
-            in_=words_raw[:].rearrange("p (n j e) -> p n j e", j=O_PER_P, e=WORD_BYTES),
-        )
-        scales = consts.tile([P, C], U8, align_bytes=64)
-        nc.vector.tensor_copy(
-            out=scales[:].rearrange("p (j n) -> p n j", j=O_PER_P),
-            in_=scales_raw[:].rearrange("p (n j) -> p n j", j=O_PER_P),
+            out=scales[:].rearrange("p (j n) -> p j n", j=O_PER_P),
+            in_=scales_raw[:].rearrange("p (n j) -> p j n", j=O_PER_P),
         )
         quantise(0)
         multiply(1)

@@ -17,13 +17,22 @@ B = 4
 I = 32
 C = 512
 X = 64
-O_PER_P = C // P
-GROUP = 8
-COLS = GROUP * X
-SIZES = [4, 4] + [GROUP] * ((B * I - GROUP) // GROUP)
-STARTS = [sum(SIZES[:g]) for g in range(len(SIZES))]
-ROUNDS = len(SIZES)
+CHUNK = 8
+COLS = CHUNK * X
 WORD_BYTES = 2
+ONE = 127
+
+NARROW_BANKS = 4
+WIDE_BANKS = 8
+HALVES = 2
+HALF_P = P // HALVES
+W_BLOCK = WORD_BYTES * HALF_P
+
+NARROW_SIZES = [4, 4] + [CHUNK] * 7
+NARROW_TOTAL = sum(NARROW_SIZES)
+WIDE_SIZE = HALVES * CHUNK
+WIDE_ROUNDS = (B * I - NARROW_TOTAL) // WIDE_SIZE
+SORT_WIDE_AT = 2
 
 FLOPS = 2 * C * C * B * I * X
 
@@ -33,13 +42,28 @@ def tile_rpn_modulator_pb_kernel(tc, q, feats, po_w_words, po_w_scales, po_b, ou
     mult = mybir.AluOpType.mult
     identity_fn = mybir.ActivationFunctionType.Identity
 
+    chunks = []
+    rounds = []
+    for n in NARROW_SIZES:
+        first = sum(size for row, size in chunks)
+        rounds.append((False, first, [len(chunks)]))
+        chunks.append((first, n))
+    for s in range(WIDE_ROUNDS):
+        first = NARROW_TOTAL + WIDE_SIZE * s
+        rounds.append((True, first, [len(chunks), len(chunks) + 1]))
+        chunks.extend([(first, CHUNK), (first + CHUNK, CHUNK)])
+
+    def chunks_of(k):
+        return rounds[k][2] if k < len(rounds) else []
+
     with ExitStack() as ctx:
         ctx.enter_context(tc.manual_schedule())
         consts = ctx.enter_context(tc.tile_pool(name="consts", bufs=1))
-        m_pool = ctx.enter_context(tc.tile_pool(name="m_pool", bufs=3))
-        code_pool = ctx.enter_context(tc.tile_pool(name="code_pool", bufs=4))
-        result_pool = ctx.enter_context(tc.tile_pool(name="result_pool", bufs=4))
-        psum = ctx.enter_context(tc.psum_pool(name="psum", bufs=2 * O_PER_P))
+        m_pool = ctx.enter_context(tc.tile_pool(name="m_pool", bufs=6))
+        code_pool = ctx.enter_context(tc.tile_pool(name="code_pool", bufs=6))
+        narrow_pool = ctx.enter_context(tc.tile_pool(name="narrow_pool", bufs=4))
+        wide_pool = ctx.enter_context(tc.tile_pool(name="wide_pool", bufs=3))
+        psum = ctx.enter_context(tc.psum_pool(name="psum", bufs=WIDE_BANKS))
 
         scales_raw = consts.tile([P, C], U8, align_bytes=64)
         nc.vector.memset(scales_raw[:].bitcast(I32), 0)
@@ -61,8 +85,14 @@ def tile_rpn_modulator_pb_kernel(tc, q, feats, po_w_words, po_w_scales, po_b, ou
             out=f_raw[:, 1:B].rearrange("p b t x -> p b (t x)"),
             in_=feats[1:B].rearrange("b (p t) y x -> p b (t y x)", t=PACK),
         )
-        bias_bf = consts.tile([P, O_PER_P], BF16)
-        nc.scalar.dma_start(out=bias_bf[:], in_=po_b.rearrange("(p j) -> p j", j=O_PER_P))
+        narrow_bias_bf = consts.tile([P, NARROW_BANKS], BF16)
+        nc.scalar.dma_start(out=narrow_bias_bf[:], in_=po_b.rearrange("(p j) -> p j", j=NARROW_BANKS))
+        wide_bias_bf = consts.tile([P, WIDE_BANKS], BF16)
+        for h in range(HALVES):
+            nc.scalar.dma_start(
+                out=wide_bias_bf[HALF_P * h : HALF_P * (h + 1), :],
+                in_=po_b.rearrange("(p j) -> p j", j=WIDE_BANKS),
+            )
 
         warm = consts.tile([P, 2], F32)
         nc.vector.memset(warm[:], 0.0)
@@ -70,106 +100,167 @@ def tile_rpn_modulator_pb_kernel(tc, q, feats, po_w_words, po_w_scales, po_b, ou
 
         ident = consts.tile([P, P], F32)
         make_identity(nc, ident[:])
-        bias = consts.tile([P, O_PER_P], F32)
-        nc.gpsimd.tensor_copy(out=bias[:], in_=bias_bf[:])
+        narrow_bias = consts.tile([P, NARROW_BANKS], F32)
+        nc.gpsimd.tensor_copy(out=narrow_bias[:], in_=narrow_bias_bf[:])
+        wide_bias = consts.tile([P, WIDE_BANKS], F32)
+        nc.gpsimd.tensor_copy(out=wide_bias[:], in_=wide_bias_bf[:])
 
-        words = consts.tile([P, WORD_BYTES * C], U8, align_bytes=64)
-        scales = consts.tile([P, C], U8, align_bytes=64)
+        narrow_words = consts.tile([P, WORD_BYTES * C], U8, align_bytes=64)
+        narrow_scales = consts.tile([P, C], U8, align_bytes=64)
+        wide_words = consts.tile([P, (2 * WIDE_BANKS + 1) * W_BLOCK], U8, align_bytes=64)
+        nc.vector.memset(wide_words[:].bitcast(I32), 0)
+        wide_scales = consts.tile([P, (WIDE_BANKS + 2) * HALF_P], U8, align_bytes=64)
+        nc.gpsimd.memset(wide_scales[:], ONE)
 
-        def sort_words(j0, j1):
+        def sort_narrow_words(j0, j1):
             nc.vector.tensor_copy(
-                out=words[:, WORD_BYTES * P * j0 : WORD_BYTES * P * j1].rearrange(
+                out=narrow_words[:, WORD_BYTES * P * j0 : WORD_BYTES * P * j1].rearrange(
                     "p (j n e) -> p j n e", j=j1 - j0, e=WORD_BYTES
                 ),
-                in_=words_raw[:].rearrange("p (n j e) -> p j n e", j=O_PER_P, e=WORD_BYTES)[:, j0:j1],
+                in_=words_raw[:].rearrange("p (n j e) -> p j n e", j=NARROW_BANKS, e=WORD_BYTES)[:, j0:j1],
             )
 
-        sort_words(0, 2)
-        sort_words(2, 4)
+        def sort_narrow_scales():
+            nc.vector.tensor_copy(
+                out=narrow_scales[:].rearrange("p (j n) -> p j n", j=NARROW_BANKS),
+                in_=scales_raw[:].rearrange("p (n j) -> p j n", j=NARROW_BANKS),
+            )
+
+        def sort_wide():
+            nc.vector.tensor_copy(
+                out=wide_words[:, W_BLOCK : (2 * WIDE_BANKS + 1) * W_BLOCK].rearrange(
+                    "p (j z n e) -> p j z n e", j=WIDE_BANKS, z=2, e=WORD_BYTES
+                )[:, :, 0],
+                in_=words_raw[:].rearrange("p (n j e) -> p j n e", j=WIDE_BANKS, e=WORD_BYTES),
+            )
+            nc.vector.tensor_copy(
+                out=wide_scales[:, HALF_P : HALF_P * (WIDE_BANKS + 1)].rearrange("p (j n) -> p j n", j=WIDE_BANKS),
+                in_=scales_raw[:].rearrange("p (n j) -> p j n", j=WIDE_BANKS),
+            )
+
+        sort_narrow_words(0, 2)
+        sort_narrow_words(2, 4)
 
         q_pairs = q_sb[:].bitcast(F32)
         qT_ps = psum.tile([P, COLS], F32, name="acc")
         for u in range(2):
             nc.tensor.transpose(qT_ps[:, P * u : P * (u + 1)], q_pairs[:, u : C // 2 : 2], ident[:])
+        turned = qT_ps[:, 0 : 2 * P].rearrange("p (u r) -> p u r", u=2)
         qT = consts.tile([P, B * I, PACK], BF16)
+        qT_words = qT[:].rearrange("p r t -> p (r t)").bitcast(F32)
         nc.vector.tensor_copy(
-            out=qT[:].rearrange("p r t -> p (r t)").bitcast(F32).rearrange("p (r u) -> p r u", u=2),
-            in_=qT_ps[:, 0 : 2 * P].rearrange("p (u r) -> p r u", u=2),
+            out=qT_words[:, 0 : 2 * NARROW_TOTAL].rearrange("p (r u) -> p r u", u=2),
+            in_=turned[:, :, 0:NARROW_TOTAL].rearrange("p u r -> p r u"),
         )
         f4 = consts.tile([P, B, X, PACK], BF16)
-        for b in range(B):
+
+        def regroup_feats(b):
             nc.scalar.copy(out=f4[:, b], in_=f_raw[:, b].rearrange("p t x -> p x t"))
 
-        out_v = out.rearrange("b i (p j) y x -> b p i (j y x)", j=O_PER_P)
+        regroup_feats(0)
+        for h in range(HALVES):
+            nc.scalar.copy(
+                out=qT_words[:, 2 * NARROW_TOTAL : 2 * B * I].rearrange(
+                    "p (s h n u) -> p h s n u", h=HALVES, n=CHUNK, u=2
+                )[:, h],
+                in_=turned[:, :, NARROW_TOTAL : B * I].rearrange(
+                    "p u (s n h) -> p h s n u", n=CHUNK, h=HALVES
+                )[:, h],
+            )
+        for b in range(1, B):
+            regroup_feats(b)
+
+        narrow_out = out.rearrange("b i (p j) y x -> b p i (j y x)", j=NARROW_BANKS)
+        wide_out = out.rearrange("b (n h) (p j) y x -> b (h p) n (j y x)", h=HALVES, j=WIDE_BANKS)
 
         m_bf = {}
         m_codes = {}
         m_scales = {}
         acc = {}
 
-        def multiply(g):
-            r0, n = STARTS[g], SIZES[g]
-            m_bf[g] = m_pool.tile([P, GROUP, X, PACK], BF16, name="m_bf", align_bytes=64)
+        def multiply(c):
+            row, n = chunks[c]
+            m_bf[c] = m_pool.tile([P, CHUNK, X, PACK], BF16, name="m_bf", align_bytes=64)
             nc.vector.tensor_tensor(
-                out=m_bf[g][:, 0:n],
-                in0=qT[:, r0 : r0 + n, :].unsqueeze(2).to_broadcast([P, n, X, PACK]),
-                in1=f4[:, r0 // I].unsqueeze(1).to_broadcast([P, n, X, PACK]),
+                out=m_bf[c][:, 0:n],
+                in0=qT[:, row : row + n, :].unsqueeze(2).to_broadcast([P, n, X, PACK]),
+                in1=f4[:, row // I].unsqueeze(1).to_broadcast([P, n, X, PACK]),
                 op=mult,
             )
 
-        def quantise(g):
-            m_codes[g] = code_pool.tile([P, COLS], U32, name="m_codes", align_bytes=64)
-            m_scales[g] = code_pool.tile([P, COLS], U8, name="m_scales", align_bytes=64)
-            cols = X * SIZES[g]
+        def quantise(c):
+            n = chunks[c][1]
+            m_codes[c] = code_pool.tile([P, COLS], U32, name="m_codes", align_bytes=64)
+            m_scales[c] = code_pool.tile([P, COLS], U8, name="m_scales", align_bytes=64)
             nc.vector.quantize_mx(
-                out=m_codes[g][:, 0:cols].bitcast(FP8X4),
-                scales=m_scales[g][:, 0:cols],
-                in_=m_bf[g][:, 0 : SIZES[g]].rearrange("p i x t -> p (i x t)"),
+                out=m_codes[c][:, 0 : X * n].bitcast(FP8X4),
+                scales=m_scales[c][:, 0 : X * n],
+                in_=m_bf[c][:, 0:n].rearrange("p i x t -> p (i x t)"),
             )
 
-        def products(g):
-            cols = X * SIZES[g]
-            for j in range(O_PER_P):
-                acc[g, j] = psum.tile([P, COLS], F32, name="acc")
+        def fill(k, j):
+            wide, first, ids = rounds[k]
+            acc[k, j] = psum.tile([P, COLS], F32, name="acc")
+            for h, c in enumerate(ids):
+                cols = X * chunks[c][1]
+                if wide:
+                    w0 = W_BLOCK * (2 * j + 1 - h)
+                    s0 = HALF_P * (j + 1 - h)
+                    lhsT = wide_words[:, w0 : w0 + HALVES * W_BLOCK]
+                    lhsT_scale = wide_scales[:, s0 : s0 + P]
+                else:
+                    lhsT = narrow_words[:, WORD_BYTES * P * j : WORD_BYTES * P * (j + 1)]
+                    lhsT_scale = narrow_scales[:, P * j : P * (j + 1)]
                 nc.tensor.matmul_mx(
-                    out=acc[g, j][:, 0:cols],
-                    lhsT=words[:, WORD_BYTES * P * j : WORD_BYTES * P * (j + 1)].bitcast(FP4X4),
-                    lhsT_scale=scales[:, P * j : P * (j + 1)],
-                    rhs=m_codes[g][:, 0:cols].bitcast(FP8X4),
-                    rhs_scale=m_scales[g][:, 0:cols],
-                    start=True,
-                    stop=True,
+                    out=acc[k, j][:, 0:cols],
+                    lhsT=lhsT.bitcast(FP4X4),
+                    lhsT_scale=lhsT_scale,
+                    rhs=m_codes[c][:, 0:cols].bitcast(FP8X4),
+                    rhs_scale=m_scales[c][:, 0:cols],
+                    start=(h == 0),
+                    stop=(h == len(ids) - 1),
                 )
 
-        def empty_and_store(g):
-            r0, n = STARTS[g], SIZES[g]
-            result = result_pool.tile([P, GROUP, O_PER_P, X], F32, name="result")
-            for j in range(O_PER_P):
-                bank = acc[g, j][:, 0 : X * n].rearrange("p (i x) -> p i x", x=X)
+        def empty(k, j, result, n):
+            wide = rounds[k][0]
+            bank = acc[k, j][:, 0 : X * n].rearrange("p (i x) -> p i x", x=X)
+            if wide and j == WIDE_BANKS - 1:
+                nc.vector.tensor_scalar_add(out=result[:, 0:n, j, :], in0=bank, scalar1=wide_bias[:, j : j + 1])
+            else:
+                bias = wide_bias if wide else narrow_bias
                 nc.scalar.activation(
-                    out=result[:, 0:n, j, :], in_=bank, func=identity_fn,
-                    bias=bias[:, j : j + 1], scale=1.0,
+                    out=result[:, 0:n, j, :], in_=bank, func=identity_fn, bias=bias[:, j : j + 1], scale=1.0
                 )
-            nc.sync.dma_start(
-                out=out_v[r0 // I][:, r0 % I : r0 % I + n, :],
-                in_=result[:, 0:n].rearrange("p i j x -> p i (j x)"),
-            )
 
         multiply(0)
-        nc.vector.tensor_copy(
-            out=scales[:].rearrange("p (j n) -> p j n", j=O_PER_P),
-            in_=scales_raw[:].rearrange("p (n j) -> p j n", j=O_PER_P),
-        )
+        sort_narrow_scales()
         quantise(0)
         multiply(1)
-        products(0)
-        quantise(1)
-        multiply(2)
-        for g in range(ROUNDS):
-            if g + 1 < ROUNDS:
-                products(g + 1)
-            if g + 2 < ROUNDS:
-                quantise(g + 2)
-            if g + 3 < ROUNDS:
-                multiply(g + 3)
-            empty_and_store(g)
+        for j in range(NARROW_BANKS):
+            fill(0, j)
+        for k, (wide, first, ids) in enumerate(rounds):
+            next_wide = k + 1 < len(rounds) and rounds[k + 1][0]
+            for c in chunks_of(k + 1):
+                quantise(c)
+            if not wide and k + 1 < len(rounds):
+                for j in range(NARROW_BANKS):
+                    fill(k + 1, j)
+            if k == SORT_WIDE_AT:
+                sort_wide()
+            for c in chunks_of(k + 2):
+                multiply(c)
+            n = chunks[ids[0]][1]
+            if wide:
+                result = wide_pool.tile([P, CHUNK, WIDE_BANKS, X], F32, name="wide_result")
+            else:
+                result = narrow_pool.tile([P, CHUNK, NARROW_BANKS, X], F32, name="narrow_result")
+            for j in range(WIDE_BANKS if wide else NARROW_BANKS):
+                empty(k, j, result, n)
+                if next_wide:
+                    fill(k + 1, j if wide else NARROW_BANKS + j)
+            if wide:
+                n0 = (first % I) // HALVES
+                target = wide_out[first // I][:, n0 : n0 + n, :]
+            else:
+                target = narrow_out[first // I][:, first % I : first % I + n, :]
+            nc.sync.dma_start(out=target, in_=result[:, 0:n].rearrange("p i j x -> p i (j x)"))

@@ -76,6 +76,8 @@ def tile_rpn_modulator_pb_kernel(tc, q, feats, po_w_words, po_w_scales, po_b, ou
             out=f_raw[:, 0].rearrange("p t x -> p (t x)"),
             in_=feats[0].rearrange("(p t) y x -> p (t y x)", t=PACK),
         )
+        narrow_bias_bf = consts.tile([P, NARROW_BANKS], BF16)
+        nc.sync.dma_start(out=narrow_bias_bf[:], in_=po_b.rearrange("(p j) -> p j", j=NARROW_BANKS))
         for quad in range(4):
             nc.sync.dma_start(
                 out=scales_raw[32 * quad : 32 * quad + 4, :].bitcast(I32),
@@ -85,11 +87,9 @@ def tile_rpn_modulator_pb_kernel(tc, q, feats, po_w_words, po_w_scales, po_b, ou
             out=f_raw[:, 1:B].rearrange("p b t x -> p b (t x)"),
             in_=feats[1:B].rearrange("b (p t) y x -> p b (t y x)", t=PACK),
         )
-        narrow_bias_bf = consts.tile([P, NARROW_BANKS], BF16)
-        nc.scalar.dma_start(out=narrow_bias_bf[:], in_=po_b.rearrange("(p j) -> p j", j=NARROW_BANKS))
         wide_bias_bf = consts.tile([P, WIDE_BANKS], BF16)
         for h in range(HALVES):
-            nc.scalar.dma_start(
+            nc.sync.dma_start(
                 out=wide_bias_bf[HALF_P * h : HALF_P * (h + 1), :],
                 in_=po_b.rearrange("(p j) -> p j", j=WIDE_BANKS),
             )
@@ -148,16 +148,16 @@ def tile_rpn_modulator_pb_kernel(tc, q, feats, po_w_words, po_w_scales, po_b, ou
         turned = qT_ps[:, 0 : 2 * P].rearrange("p (u r) -> p u r", u=2)
         qT = consts.tile([P, B * I, PACK], BF16)
         qT_words = qT[:].rearrange("p r t -> p (r t)").bitcast(F32)
-        nc.vector.tensor_copy(
-            out=qT_words[:, 0 : 2 * NARROW_TOTAL].rearrange("p (r u) -> p r u", u=2),
-            in_=turned[:, :, 0:NARROW_TOTAL].rearrange("p u r -> p r u"),
-        )
         f4 = consts.tile([P, B, X, PACK], BF16)
 
         def regroup_feats(b):
             nc.scalar.copy(out=f4[:, b], in_=f_raw[:, b].rearrange("p t x -> p x t"))
 
         regroup_feats(0)
+        nc.scalar.copy(
+            out=qT_words[:, 0 : 2 * NARROW_TOTAL].rearrange("p (r u) -> p r u", u=2),
+            in_=turned[:, :, 0:NARROW_TOTAL].rearrange("p u r -> p r u"),
+        )
         for h in range(HALVES):
             nc.scalar.copy(
                 out=qT_words[:, 2 * NARROW_TOTAL : 2 * B * I].rearrange(

@@ -28,11 +28,12 @@ HALVES = 2
 HALF_P = P // HALVES
 W_BLOCK = WORD_BYTES * HALF_P
 
-NARROW_SIZES = [4, 4] + [CHUNK] * 7
+NARROW_SIZES = [4, 4] + [CHUNK] * 5
 NARROW_TOTAL = sum(NARROW_SIZES)
 WIDE_SIZE = HALVES * CHUNK
 WIDE_ROUNDS = (B * I - NARROW_TOTAL) // WIDE_SIZE
 SORT_WIDE_AT = 2
+VECTOR_BANKS = (3, 7)
 
 FLOPS = 2 * C * C * B * I * X
 
@@ -53,8 +54,9 @@ def tile_rpn_modulator_pb_kernel(tc, q, feats, po_w_words, po_w_scales, po_b, ou
         rounds.append((True, first, [len(chunks), len(chunks) + 1]))
         chunks.extend([(first, CHUNK), (first + CHUNK, CHUNK)])
 
-    def chunks_of(k):
-        return rounds[k][2] if k < len(rounds) else []
+    groups = [[k, k + 1] for k in range(1, len(NARROW_SIZES), 2)]
+    groups.extend([[k] for k in range(len(NARROW_SIZES), len(rounds))])
+    group_that_starts_with = dict((group[0], group) for group in groups)
 
     with ExitStack() as ctx:
         ctx.enter_context(tc.manual_schedule())
@@ -224,7 +226,7 @@ def tile_rpn_modulator_pb_kernel(tc, q, feats, po_w_words, po_w_scales, po_b, ou
         def empty(k, j, result, n):
             wide = rounds[k][0]
             bank = acc[k, j][:, 0 : X * n].rearrange("p (i x) -> p i x", x=X)
-            if wide and j == WIDE_BANKS - 1:
+            if wide and j in VECTOR_BANKS:
                 nc.vector.tensor_scalar_add(out=result[:, 0:n, j, :], in0=bank, scalar1=wide_bias[:, j : j + 1])
             else:
                 bias = wide_bias if wide else narrow_bias
@@ -232,23 +234,26 @@ def tile_rpn_modulator_pb_kernel(tc, q, feats, po_w_words, po_w_scales, po_b, ou
                     out=result[:, 0:n, j, :], in_=bank, func=identity_fn, bias=bias[:, j : j + 1], scale=1.0
                 )
 
+        def prepare(k):
+            ids = [c for r in group_that_starts_with.get(k, []) for c in rounds[r][2]]
+            for c in ids:
+                multiply(c)
+            for c in ids:
+                quantise(c)
+
         multiply(0)
         sort_narrow_scales()
         quantise(0)
-        multiply(1)
         for j in range(NARROW_BANKS):
             fill(0, j)
         for k, (wide, first, ids) in enumerate(rounds):
             next_wide = k + 1 < len(rounds) and rounds[k + 1][0]
-            for c in chunks_of(k + 1):
-                quantise(c)
+            prepare(k + 1)
             if not wide and k + 1 < len(rounds):
                 for j in range(NARROW_BANKS):
                     fill(k + 1, j)
             if k == SORT_WIDE_AT:
                 sort_wide()
-            for c in chunks_of(k + 2):
-                multiply(c)
             n = chunks[ids[0]][1]
             if wide:
                 result = wide_pool.tile([P, CHUNK, WIDE_BANKS, X], F32, name="wide_result")

@@ -34,6 +34,8 @@ WIDE_SIZE = HALVES * CHUNK
 WIDE_ROUNDS = (B * I - NARROW_TOTAL) // WIDE_SIZE
 SORT_WIDE_AT = 2
 VECTOR_BANKS = (3, 7)
+WARM_BEFORE = 4
+WARM_BETWEEN = 6
 
 FLOPS = 2 * C * C * B * I * X
 
@@ -69,6 +71,8 @@ def tile_rpn_modulator_pb_kernel(tc, q, feats, po_w_words, po_w_scales, po_b, ou
 
         scales_raw = consts.tile([P, C], U8, align_bytes=64)
         nc.vector.memset(scales_raw[:].bitcast(I32), 0)
+        zeros = consts.tile([P, COLS], BF16)
+        nc.vector.memset(zeros[:], 0.0)
         words_raw = consts.tile([P, WORD_BYTES * C], U8, align_bytes=64)
         nc.sync.dma_start(out=words_raw[:].bitcast(I32), in_=po_w_words[0].bitcast(I32))
         q_sb = consts.tile([P, C], BF16)
@@ -143,10 +147,18 @@ def tile_rpn_modulator_pb_kernel(tc, q, feats, po_w_words, po_w_scales, po_b, ou
         sort_narrow_words(0, 2)
         sort_narrow_words(2, 4)
 
+        dummy_ps = psum.tile([P, COLS], F32, name="acc")
+
+        def dummies(count):
+            for d in range(count):
+                nc.tensor.matmul(out=dummy_ps[:], lhsT=zeros[:, 0:P], rhs=zeros[:], start=True, stop=True)
+
+        dummies(WARM_BEFORE)
         q_pairs = q_sb[:].bitcast(F32)
         qT_ps = psum.tile([P, COLS], F32, name="acc")
         for u in range(2):
             nc.tensor.transpose(qT_ps[:, P * u : P * (u + 1)], q_pairs[:, u : C // 2 : 2], ident[:])
+        dummies(WARM_BETWEEN)
         turned = qT_ps[:, 0 : 2 * P].rearrange("p (u r) -> p u r", u=2)
         qT = consts.tile([P, B * I, PACK], BF16)
         qT_words = qT[:].rearrange("p r t -> p (r t)").bitcast(F32)

@@ -34,6 +34,7 @@ WIDE_SIZE = HALVES * CHUNK
 WIDE_ROUNDS = (B * I - NARROW_TOTAL) // WIDE_SIZE
 SORT_WIDE_AT = 2
 VECTOR_BANKS = (3, 7)
+HALVED_ROUNDS = (2, 3, 4)
 WARM_BEFORE = 4
 WARM_BETWEEN = 6
 
@@ -235,15 +236,17 @@ def tile_rpn_modulator_pb_kernel(tc, q, feats, po_w_words, po_w_scales, po_b, ou
                     stop=(h == len(ids) - 1),
                 )
 
-        def empty(k, j, result, n):
+        def empty(k, j, result, i0, n):
             wide = rounds[k][0]
-            bank = acc[k, j][:, 0 : X * n].rearrange("p (i x) -> p i x", x=X)
+            bank = acc[k, j][:, X * i0 : X * (i0 + n)].rearrange("p (i x) -> p i x", x=X)
             if wide and j in VECTOR_BANKS:
-                nc.vector.tensor_scalar_add(out=result[:, 0:n, j, :], in0=bank, scalar1=wide_bias[:, j : j + 1])
+                nc.vector.tensor_scalar_add(
+                    out=result[:, i0 : i0 + n, j, :], in0=bank, scalar1=wide_bias[:, j : j + 1]
+                )
             else:
                 bias = wide_bias if wide else narrow_bias
                 nc.scalar.activation(
-                    out=result[:, 0:n, j, :], in_=bank, func=identity_fn, bias=bias[:, j : j + 1], scale=1.0
+                    out=result[:, i0 : i0 + n, j, :], in_=bank, func=identity_fn, bias=bias[:, j : j + 1], scale=1.0
                 )
 
         def prepare(k):
@@ -271,13 +274,16 @@ def tile_rpn_modulator_pb_kernel(tc, q, feats, po_w_words, po_w_scales, po_b, ou
                 result = wide_pool.tile([P, CHUNK, WIDE_BANKS, X], F32, name="wide_result")
             else:
                 result = narrow_pool.tile([P, CHUNK, NARROW_BANKS, X], F32, name="narrow_result")
-            for j in range(WIDE_BANKS if wide else NARROW_BANKS):
-                empty(k, j, result, n)
-                if next_wide:
-                    fill(k + 1, j if wide else NARROW_BANKS + j)
-            if wide:
-                n0 = (first % I) // HALVES
-                target = wide_out[first // I][:, n0 : n0 + n, :]
-            else:
-                target = narrow_out[first // I][:, first % I : first % I + n, :]
-            nc.sync.dma_start(out=target, in_=result[:, 0:n].rearrange("p i j x -> p i (j x)"))
+            parts = 2 if k in HALVED_ROUNDS else 1
+            step = n // parts
+            for i0 in range(0, n, step):
+                for j in range(WIDE_BANKS if wide else NARROW_BANKS):
+                    empty(k, j, result, i0, step)
+                    if next_wide:
+                        fill(k + 1, j if wide else NARROW_BANKS + j)
+                if wide:
+                    n0 = (first % I) // HALVES
+                    target = wide_out[first // I][:, n0 : n0 + n, :]
+                else:
+                    target = narrow_out[first // I][:, first % I + i0 : first % I + i0 + step, :]
+                nc.sync.dma_start(out=target, in_=result[:, i0 : i0 + step].rearrange("p i j x -> p i (j x)"))

@@ -70,6 +70,11 @@ def tile_rpn_modulator_pb_kernel(tc, q, feats, po_w_words, po_w_scales, po_b, ou
         wide_pool = ctx.enter_context(tc.tile_pool(name="wide_pool", bufs=3))
         psum = ctx.enter_context(tc.psum_pool(name="psum", bufs=WIDE_BANKS))
 
+        wide_scales = consts.tile([P, (WIDE_BANKS + 2) * HALF_P], U8, align_bytes=64)
+        nc.gpsimd.memset(wide_scales[:], ONE)
+        ident = consts.tile([P, P], F32)
+        make_identity(nc, ident[:])
+
         scales_raw = consts.tile([P, C], U8, align_bytes=64)
         nc.vector.memset(scales_raw[:].bitcast(I32), 0)
         zeros = consts.tile([P, COLS], BF16)
@@ -83,8 +88,8 @@ def tile_rpn_modulator_pb_kernel(tc, q, feats, po_w_words, po_w_scales, po_b, ou
             out=f_raw[:, 0].rearrange("p t x -> p (t x)"),
             in_=feats[0].rearrange("(p t) y x -> p (t y x)", t=PACK),
         )
-        narrow_bias_bf = consts.tile([P, NARROW_BANKS], BF16)
-        nc.sync.dma_start(out=narrow_bias_bf[:], in_=po_b.rearrange("(p j) -> p j", j=NARROW_BANKS))
+        narrow_bias = consts.tile([P, NARROW_BANKS], BF16)
+        nc.sync.dma_start(out=narrow_bias[:], in_=po_b.rearrange("(p j) -> p j", j=NARROW_BANKS))
         for quad in range(4):
             nc.sync.dma_start(
                 out=scales_raw[32 * quad : 32 * quad + 4, :].bitcast(I32),
@@ -94,10 +99,10 @@ def tile_rpn_modulator_pb_kernel(tc, q, feats, po_w_words, po_w_scales, po_b, ou
             out=f_raw[:, 1:B].rearrange("p b t x -> p b (t x)"),
             in_=feats[1:B].rearrange("b (p t) y x -> p b (t y x)", t=PACK),
         )
-        wide_bias_bf = consts.tile([P, WIDE_BANKS], BF16)
+        wide_bias = consts.tile([P, WIDE_BANKS], BF16)
         for h in range(HALVES):
             nc.sync.dma_start(
-                out=wide_bias_bf[HALF_P * h : HALF_P * (h + 1), :],
+                out=wide_bias[HALF_P * h : HALF_P * (h + 1), :],
                 in_=po_b.rearrange("(p j) -> p j", j=WIDE_BANKS),
             )
 
@@ -105,19 +110,10 @@ def tile_rpn_modulator_pb_kernel(tc, q, feats, po_w_words, po_w_scales, po_b, ou
         nc.vector.memset(warm[:], 0.0)
         nc.scalar.activation(out=warm[:, 1:2], in_=warm[:, 0:1], func=identity_fn, scale=1.0)
 
-        ident = consts.tile([P, P], F32)
-        make_identity(nc, ident[:])
-        narrow_bias = consts.tile([P, NARROW_BANKS], F32)
-        nc.gpsimd.tensor_copy(out=narrow_bias[:], in_=narrow_bias_bf[:])
-        wide_bias = consts.tile([P, WIDE_BANKS], F32)
-        nc.gpsimd.tensor_copy(out=wide_bias[:], in_=wide_bias_bf[:])
-
         narrow_words = consts.tile([P, WORD_BYTES * C], U8, align_bytes=64)
         narrow_scales = consts.tile([P, C], U8, align_bytes=64)
         wide_words = consts.tile([P, (2 * WIDE_BANKS + 1) * W_BLOCK], U8, align_bytes=64)
         nc.vector.memset(wide_words[:].bitcast(I32), 0)
-        wide_scales = consts.tile([P, (WIDE_BANKS + 2) * HALF_P], U8, align_bytes=64)
-        nc.gpsimd.memset(wide_scales[:], ONE)
 
         def sort_narrow_words(j0, j1):
             nc.vector.tensor_copy(

@@ -21,6 +21,7 @@ CHUNK = 8
 COLS = CHUNK * X
 WORD_BYTES = 2
 ONE = 127
+FOUR_ONES = ONE * (1 + 256 + 256 ** 2 + 256 ** 3)
 
 NARROW_BANKS = 4
 WIDE_BANKS = 8
@@ -70,8 +71,6 @@ def tile_rpn_modulator_pb_kernel(tc, q, feats, po_w_words, po_w_scales, po_b, ou
         wide_pool = ctx.enter_context(tc.tile_pool(name="wide_pool", bufs=3))
         psum = ctx.enter_context(tc.psum_pool(name="psum", bufs=WIDE_BANKS))
 
-        wide_scales = consts.tile([P, (WIDE_BANKS + 2) * HALF_P], U8, align_bytes=64)
-        nc.gpsimd.memset(wide_scales[:], ONE)
         ident = consts.tile([P, P], F32)
         make_identity(nc, ident[:])
 
@@ -114,6 +113,8 @@ def tile_rpn_modulator_pb_kernel(tc, q, feats, po_w_words, po_w_scales, po_b, ou
         narrow_scales = consts.tile([P, C], U8, align_bytes=64)
         wide_words = consts.tile([P, (2 * WIDE_BANKS + 1) * W_BLOCK], U8, align_bytes=64)
         nc.vector.memset(wide_words[:].bitcast(I32), 0)
+        wide_scales = consts.tile([P, (WIDE_BANKS + 2) * HALF_P], U8, align_bytes=64)
+        nc.vector.memset(wide_scales[:].bitcast(I32), FOUR_ONES)
 
         def sort_narrow_words(j0, j1):
             nc.vector.tensor_copy(

@@ -35,6 +35,7 @@ WIDE_SIZE = HALVES * CHUNK
 WIDE_ROUNDS = (B * I - NARROW_TOTAL) // WIDE_SIZE
 SORT_WIDE_AT = 2
 VECTOR_BANKS = (3, 7)
+FIRST_WIDE_VECTOR_BANKS = (3, 5, 7)
 HALVED_ROUNDS = (2, 3, 4)
 WARM_BEFORE = 4
 WARM_BETWEEN = 6
@@ -210,10 +211,13 @@ def tile_rpn_modulator_pb_kernel(tc, q, feats, po_w_words, po_w_scales, po_b, ou
                 in_=m_bf[c][:, 0:n].rearrange("p i x t -> p (i x t)"),
             )
 
-        def fill(k, j):
+        def fill(k, j, passes=(0, 1)):
             wide, first, ids = rounds[k]
-            acc[k, j] = psum.tile([P, COLS], F32, name="acc")
+            if 0 in passes:
+                acc[k, j] = psum.tile([P, COLS], F32, name="acc")
             for h, c in enumerate(ids):
+                if h not in passes:
+                    continue
                 cols = X * chunks[c][1]
                 if wide:
                     w0 = W_BLOCK * (2 * j + 1 - h)
@@ -236,7 +240,7 @@ def tile_rpn_modulator_pb_kernel(tc, q, feats, po_w_words, po_w_scales, po_b, ou
         def empty(k, j, result, i0, n):
             wide = rounds[k][0]
             bank = acc[k, j][:, X * i0 : X * (i0 + n)].rearrange("p (i x) -> p i x", x=X)
-            if wide and j in VECTOR_BANKS:
+            if wide and j in (FIRST_WIDE_VECTOR_BANKS if k == len(NARROW_SIZES) else VECTOR_BANKS):
                 nc.vector.tensor_scalar_add(
                     out=result[:, i0 : i0 + n, j, :], in0=bank, scalar1=wide_bias[:, j : j + 1]
                 )
@@ -261,7 +265,11 @@ def tile_rpn_modulator_pb_kernel(tc, q, feats, po_w_words, po_w_scales, po_b, ou
         for k, (wide, first, ids) in enumerate(rounds):
             next_wide = k + 1 < len(rounds) and rounds[k + 1][0]
             prepare(k + 1)
-            if not wide and k + 1 < len(rounds):
+            if next_wide and not wide:
+                for h in range(HALVES):
+                    for j in range(NARROW_BANKS):
+                        fill(k + 1, j, (h,))
+            elif not wide and k + 1 < len(rounds):
                 for j in range(NARROW_BANKS):
                     fill(k + 1, j)
             if k == SORT_WIDE_AT:

@@ -72,11 +72,14 @@ def tile_rpn_modulator_pb_kernel(tc, q, feats, po_w_words, po_w_scales, po_b, ou
         wide_pool = ctx.enter_context(tc.tile_pool(name="wide_pool", bufs=3))
         psum = ctx.enter_context(tc.psum_pool(name="psum", bufs=WIDE_BANKS))
 
-        ident = consts.tile([P, P], F32)
-        make_identity(nc, ident[:])
-
+        warm = consts.tile([P, 2], F32)
+        nc.vector.memset(warm[:], 0.0)
         scales_raw = consts.tile([P, C], U8, align_bytes=64)
         nc.vector.memset(scales_raw[:].bitcast(I32), 0)
+        ident = consts.tile([P, P], F32)
+        nc.vector.memset(ident[:], 0.0)
+        make_identity(nc, ident[:], nomemset=True)
+
         zeros = consts.tile([P, COLS], BF16)
         nc.vector.memset(zeros[:], 0.0)
         words_raw = consts.tile([P, WORD_BYTES * C], U8, align_bytes=64)
@@ -106,8 +109,6 @@ def tile_rpn_modulator_pb_kernel(tc, q, feats, po_w_words, po_w_scales, po_b, ou
                 in_=po_b.rearrange("(p j) -> p j", j=WIDE_BANKS),
             )
 
-        warm = consts.tile([P, 2], F32)
-        nc.vector.memset(warm[:], 0.0)
         nc.scalar.activation(out=warm[:, 1:2], in_=warm[:, 0:1], func=identity_fn, scale=1.0)
 
         narrow_words = consts.tile([P, WORD_BYTES * C], U8, align_bytes=64)

from contextlib import ExitStack

import concourse.mybir as mybir
from concourse.masks import make_identity

F32 = mybir.dt.float32
BF16 = mybir.dt.bfloat16
I32 = mybir.dt.int32
U32 = mybir.dt.uint32
U8 = mybir.dt.uint8
FP8X4 = mybir.dt.float8_e4m3fn_x4
FP4X4 = mybir.dt.float4_e2m1fn_x4

P = 128
PACK = 4
B = 4
I = 32
C = 512
X = 64
CHUNK = 8
COLS = CHUNK * X
WORD_BYTES = 2
ONE = 127
FOUR_ONES = ONE * (1 + 256 + 256 ** 2 + 256 ** 3)

NARROW_BANKS = 4
WIDE_BANKS = 8
HALVES = 2
HALF_P = P // HALVES
W_BLOCK = WORD_BYTES * HALF_P

NARROW_SIZES = [4, 4] + [CHUNK] * 5
NARROW_TOTAL = sum(NARROW_SIZES)
WIDE_SIZE = HALVES * CHUNK
WIDE_ROUNDS = (B * I - NARROW_TOTAL) // WIDE_SIZE
SORT_WIDE_AT = 2
VECTOR_BANKS = (3, 7)
FIRST_WIDE_VECTOR_BANKS = (3, 5, 7)
HALVED_ROUNDS = (2, 3, 4)
WARM_BEFORE = 4
WARM_BETWEEN = 6

FLOPS = 2 * C * C * B * I * X


def tile_rpn_modulator_pb_kernel(tc, q, feats, po_w_words, po_w_scales, po_b, out):
    nc = tc.nc
    mult = mybir.AluOpType.mult
    identity_fn = mybir.ActivationFunctionType.Identity

    chunks = []
    rounds = []
    for n in NARROW_SIZES:
        first = sum(size for row, size in chunks)
        rounds.append((False, first, [len(chunks)]))
        chunks.append((first, n))
    for s in range(WIDE_ROUNDS):
        first = NARROW_TOTAL + WIDE_SIZE * s
        rounds.append((True, first, [len(chunks), len(chunks) + 1]))
        chunks.extend([(first, CHUNK), (first + CHUNK, CHUNK)])

    groups = [[k, k + 1] for k in range(1, len(NARROW_SIZES), 2)]
    groups.extend([[k] for k in range(len(NARROW_SIZES), len(rounds))])
    group_that_starts_with = dict((group[0], group) for group in groups)

    with ExitStack() as ctx:
        ctx.enter_context(tc.manual_schedule())
        consts = ctx.enter_context(tc.tile_pool(name="consts", bufs=1))
        m_pool = ctx.enter_context(tc.tile_pool(name="m_pool", bufs=6))
        code_pool = ctx.enter_context(tc.tile_pool(name="code_pool", bufs=6))
        narrow_pool = ctx.enter_context(tc.tile_pool(name="narrow_pool", bufs=4))
        wide_pool = ctx.enter_context(tc.tile_pool(name="wide_pool", bufs=3))
        psum = ctx.enter_context(tc.psum_pool(name="psum", bufs=WIDE_BANKS))

        warm = consts.tile([P, 2], F32)
        nc.vector.memset(warm[:], 0.0)
        scales_raw = consts.tile([P, C], U8, align_bytes=64)
        nc.vector.memset(scales_raw[:].bitcast(I32), 0)
        ident = consts.tile([P, P], F32)
        nc.vector.memset(ident[:], 0.0)
        make_identity(nc, ident[:], nomemset=True)

        zeros = consts.tile([P, COLS], BF16)
        nc.vector.memset(zeros[:], 0.0)
        words_raw = consts.tile([P, WORD_BYTES * C], U8, align_bytes=64)
        nc.sync.dma_start(out=words_raw[:].bitcast(I32), in_=po_w_words[0].bitcast(I32))
        q_sb = consts.tile([P, C], BF16)
        nc.scalar.dma_start(out=q_sb[:], in_=q.rearrange("b i c -> (b i) c"))
        f_raw = consts.tile([P, B, PACK, X], BF16)
        nc.sync.dma_start(
            out=f_raw[:, 0].rearrange("p t x -> p (t x)"),
            in_=feats[0].rearrange("(p t) y x -> p (t y x)", t=PACK),
        )
        narrow_bias = consts.tile([P, NARROW_BANKS], BF16)
        nc.sync.dma_start(out=narrow_bias[:], in_=po_b.rearrange("(p j) -> p j", j=NARROW_BANKS))
        for quad in range(4):
            nc.sync.dma_start(
                out=scales_raw[32 * quad : 32 * quad + 4, :].bitcast(I32),
                in_=po_w_scales[0, 4 * quad : 4 * quad + 4, :].bitcast(I32),
            )
        nc.scalar.dma_start(
            out=f_raw[:, 1:B].rearrange("p b t x -> p b (t x)"),
            in_=feats[1:B].rearrange("b (p t) y x -> p b (t y x)", t=PACK),
        )
        wide_bias = consts.tile([P, WIDE_BANKS], BF16)
        for h in range(HALVES):
            nc.sync.dma_start(
                out=wide_bias[HALF_P * h : HALF_P * (h + 1), :],
                in_=po_b.rearrange("(p j) -> p j", j=WIDE_BANKS),
            )

        nc.scalar.activation(out=warm[:, 1:2], in_=warm[:, 0:1], func=identity_fn, scale=1.0)

        narrow_words = consts.tile([P, WORD_BYTES * C], U8, align_bytes=64)
        narrow_scales = consts.tile([P, C], U8, align_bytes=64)
        wide_words = consts.tile([P, (2 * WIDE_BANKS + 1) * W_BLOCK], U8, align_bytes=64)
        nc.vector.memset(wide_words[:].bitcast(I32), 0)
        wide_scales = consts.tile([P, (WIDE_BANKS + 2) * HALF_P], U8, align_bytes=64)
        nc.vector.memset(wide_scales[:].bitcast(I32), FOUR_ONES)

        def sort_narrow_words(j0, j1):
            nc.vector.tensor_copy(
                out=narrow_words[:, WORD_BYTES * P * j0 : WORD_BYTES * P * j1].rearrange(
                    "p (j n e) -> p j n e", j=j1 - j0, e=WORD_BYTES
                ),
                in_=words_raw[:].rearrange("p (n j e) -> p j n e", j=NARROW_BANKS, e=WORD_BYTES)[:, j0:j1],
            )

        def sort_narrow_scales():
            nc.vector.tensor_copy(
                out=narrow_scales[:].rearrange("p (j n) -> p j n", j=NARROW_BANKS),
                in_=scales_raw[:].rearrange("p (n j) -> p j n", j=NARROW_BANKS),
            )

        def sort_wide():
            nc.vector.tensor_copy(
                out=wide_words[:, W_BLOCK : (2 * WIDE_BANKS + 1) * W_BLOCK].rearrange(
                    "p (j z n e) -> p j z n e", j=WIDE_BANKS, z=2, e=WORD_BYTES
                )[:, :, 0],
                in_=words_raw[:].rearrange("p (n j e) -> p j n e", j=WIDE_BANKS, e=WORD_BYTES),
            )
            nc.vector.tensor_copy(
                out=wide_scales[:, HALF_P : HALF_P * (WIDE_BANKS + 1)].rearrange("p (j n) -> p j n", j=WIDE_BANKS),
                in_=scales_raw[:].rearrange("p (n j) -> p j n", j=WIDE_BANKS),
            )

        sort_narrow_words(0, 2)
        sort_narrow_words(2, 4)

        dummy_ps = psum.tile([P, COLS], F32, name="acc")

        def dummies(count):
            for d in range(count):
                nc.tensor.matmul(out=dummy_ps[:], lhsT=zeros[:, 0:P], rhs=zeros[:], start=True, stop=True)

        dummies(WARM_BEFORE)
        q_pairs = q_sb[:].bitcast(F32)
        qT_ps = psum.tile([P, COLS], F32, name="acc")
        for u in range(2):
            nc.tensor.transpose(qT_ps[:, P * u : P * (u + 1)], q_pairs[:, u : C // 2 : 2], ident[:])
        dummies(WARM_BETWEEN)
        turned = qT_ps[:, 0 : 2 * P].rearrange("p (u r) -> p u r", u=2)
        qT = consts.tile([P, B * I, PACK], BF16)
        qT_words = qT[:].rearrange("p r t -> p (r t)").bitcast(F32)
        f4 = consts.tile([P, B, X, PACK], BF16)

        def regroup_feats(b):
            nc.scalar.copy(out=f4[:, b], in_=f_raw[:, b].rearrange("p t x -> p x t"))

        regroup_feats(0)
        nc.scalar.copy(
            out=qT_words[:, 0 : 2 * NARROW_TOTAL].rearrange("p (r u) -> p r u", u=2),
            in_=turned[:, :, 0:NARROW_TOTAL].rearrange("p u r -> p r u"),
        )
        for h in range(HALVES):
            nc.scalar.copy(
                out=qT_words[:, 2 * NARROW_TOTAL : 2 * B * I].rearrange(
                    "p (s h n u) -> p h s n u", h=HALVES, n=CHUNK, u=2
                )[:, h],
                in_=turned[:, :, NARROW_TOTAL : B * I].rearrange(
                    "p u (s n h) -> p h s n u", n=CHUNK, h=HALVES
                )[:, h],
            )
        for b in range(1, B):
            regroup_feats(b)

        narrow_out = out.rearrange("b i (p j) y x -> b p i (j y x)", j=NARROW_BANKS)
        wide_out = out.rearrange("b (n h) (p j) y x -> b (h p) n (j y x)", h=HALVES, j=WIDE_BANKS)

        m_bf = {}
        m_codes = {}
        m_scales = {}
        acc = {}

        def multiply(c):
            row, n = chunks[c]
            m_bf[c] = m_pool.tile([P, CHUNK, X, PACK], BF16, name="m_bf", align_bytes=64)
            nc.vector.tensor_tensor(
                out=m_bf[c][:, 0:n],
                in0=qT[:, row : row + n, :].unsqueeze(2).to_broadcast([P, n, X, PACK]),
                in1=f4[:, row // I].unsqueeze(1).to_broadcast([P, n, X, PACK]),
                op=mult,
            )

        def quantise(c):
            n = chunks[c][1]
            m_codes[c] = code_pool.tile([P, COLS], U32, name="m_codes", align_bytes=64)
            m_scales[c] = code_pool.tile([P, COLS], U8, name="m_scales", align_bytes=64)
            nc.vector.quantize_mx(
                out=m_codes[c][:, 0 : X * n].bitcast(FP8X4),
                scales=m_scales[c][:, 0 : X * n],
                in_=m_bf[c][:, 0:n].rearrange("p i x t -> p (i x t)"),
            )

        def fill(k, j, passes=(0, 1)):
            wide, first, ids = rounds[k]
            if 0 in passes:
                acc[k, j] = psum.tile([P, COLS], F32, name="acc")
            for h, c in enumerate(ids):
                if h not in passes:
                    continue
                cols = X * chunks[c][1]
                if wide:
                    w0 = W_BLOCK * (2 * j + 1 - h)
                    s0 = HALF_P * (j + 1 - h)
                    lhsT = wide_words[:, w0 : w0 + HALVES * W_BLOCK]
                    lhsT_scale = wide_scales[:, s0 : s0 + P]
                else:
                    lhsT = narrow_words[:, WORD_BYTES * P * j : WORD_BYTES * P * (j + 1)]
                    lhsT_scale = narrow_scales[:, P * j : P * (j + 1)]
                nc.tensor.matmul_mx(
                    out=acc[k, j][:, 0:cols],
                    lhsT=lhsT.bitcast(FP4X4),
                    lhsT_scale=lhsT_scale,
                    rhs=m_codes[c][:, 0:cols].bitcast(FP8X4),
                    rhs_scale=m_scales[c][:, 0:cols],
                    start=(h == 0),
                    stop=(h == len(ids) - 1),
                )

        def empty(k, j, result, i0, n):
            wide = rounds[k][0]
            bank = acc[k, j][:, X * i0 : X * (i0 + n)].rearrange("p (i x) -> p i x", x=X)
            if wide and j in (FIRST_WIDE_VECTOR_BANKS if k == len(NARROW_SIZES) else VECTOR_BANKS):
                nc.vector.tensor_scalar_add(
                    out=result[:, i0 : i0 + n, j, :], in0=bank, scalar1=wide_bias[:, j : j + 1]
                )
            else:
                bias = wide_bias if wide else narrow_bias
                nc.scalar.activation(
                    out=result[:, i0 : i0 + n, j, :], in_=bank, func=identity_fn, bias=bias[:, j : j + 1], scale=1.0
                )

        def prepare(k):
            ids = [c for r in group_that_starts_with.get(k, []) for c in rounds[r][2]]
            for c in ids:
                multiply(c)
            for c in ids:
                quantise(c)

        multiply(0)
        sort_narrow_scales()
        quantise(0)
        for j in range(NARROW_BANKS):
            fill(0, j)
        for k, (wide, first, ids) in enumerate(rounds):
            next_wide = k + 1 < len(rounds) and rounds[k + 1][0]
            prepare(k + 1)
            if next_wide and not wide:
                for h in range(HALVES):
                    for j in range(NARROW_BANKS):
                        fill(k + 1, j, (h,))
            elif not wide and k + 1 < len(rounds):
                for j in range(NARROW_BANKS):
                    fill(k + 1, j)
            if k == SORT_WIDE_AT:
                sort_wide()
            n = chunks[ids[0]][1]
            if wide:
                result = wide_pool.tile([P, CHUNK, WIDE_BANKS, X], F32, name="wide_result")
            else:
                result = narrow_pool.tile([P, CHUNK, NARROW_BANKS, X], F32, name="narrow_result")
            parts = 2 if k in HALVED_ROUNDS else 1
            step = n // parts
            for i0 in range(0, n, step):
                for j in range(WIDE_BANKS if wide else NARROW_BANKS):
                    empty(k, j, result, i0, step)
                    if next_wide:
                        fill(k + 1, j if wide else NARROW_BANKS + j)
                if wide:
                    n0 = (first % I) // HALVES
                    target = wide_out[first // I][:, n0 : n0 + n, :]
                else:
                    target = narrow_out[first // I][:, first % I + i0 : first % I + i0 + step, :]
                nc.sync.dma_start(out=target, in_=result[:, i0 : i0 + step].rearrange("p i j x -> p i (j x)"))
